import numpy as np
import ml_dtypes


def mxq(x, axis, fmt="e4m3"):
    dtype, down = {"e4m3": (ml_dtypes.float8_e4m3fn, 7), "e5m2": (ml_dtypes.float8_e5m2, 14)}[fmt]
    v = np.moveaxis(np.asarray(x, np.float32).astype(ml_dtypes.bfloat16).astype(np.float64), axis, -1)
    blocks = v.reshape(v.shape[:-1] + (-1, 32))
    amax = np.abs(blocks).max(-1, keepdims=True)
    byte = np.maximum(np.where(amax > 0, np.frexp(amax)[1] - 1 + 127, 0) - down, 1)
    scale = np.exp2(byte - 127.0)
    codes = (blocks / scale).astype(np.float32).astype(dtype).astype(np.float64)
    return np.moveaxis((codes * scale).reshape(v.shape), -1, axis)


WIDE = False


def mx_kscale(k):
    if not WIDE:
        return np.ones(k)
    levels = np.array([10, -10, 5, -5, 0])
    a = np.random.permutation(np.resize(levels, k // 512 * 4)).reshape(k // 512, 4)
    idx = np.arange(k)
    return np.exp2(a[idx // 512, idx % 128 // 32])


BF16 = ml_dtypes.bfloat16


def bf(x):
    return np.asarray(x, np.float32).astype(BF16)


def f64(x):
    return np.asarray(x).astype(np.float64)


E2M1 = np.array([0.0, 0.5, 1.0, 1.5, 2.0, 3.0, 4.0, 6.0, -0.0, -0.5, -1.0, -1.5, -2.0, -3.0, -4.0, -6.0])


def pack_weight(w, fmt):
    k, n = w.shape
    w = f64(bf(w)).reshape(k // 32, 32, n)
    amax = np.abs(w).max(1)
    if fmt == "e4m3":
        byte = np.frexp(amax)[1] - 1 + 127 - 7
    else:
        mant, ex = np.frexp(amax / 6.0)
        byte = np.where(mant > 0.5, ex, ex - 1) + 127
    byte = np.clip(np.where(amax > 0, byte, 1), 1, 254)
    scaled = (w * np.exp2(127.0 - byte)[:, None, :]).reshape(k, n).astype(np.float32)
    by_word = np.ascontiguousarray(scaled.reshape(k // 512, 128, 4, n).transpose(0, 1, 3, 2))
    if fmt == "e4m3":
        words = by_word.astype(ml_dtypes.float8_e4m3fn).view(np.uint8)
    else:
        c = by_word.astype(ml_dtypes.float4_e2m1fn).view(np.uint8) & 0xF
        words = c[..., 0::2] | (c[..., 1::2] << 4)
    return np.ascontiguousarray(words), np.ascontiguousarray(byte.astype(np.uint8).reshape(k // 512, 16, n))


def unpack_weight(words, scales, fmt):
    g, p, n, _ = words.shape
    if fmt == "e4m3":
        vals = np.ascontiguousarray(words).view(ml_dtypes.float8_e4m3fn).astype(np.float64)
    else:
        nib = np.empty((g, p, n, 4), np.uint8)
        nib[..., 0::2] = words & 0xF
        nib[..., 1::2] = words >> 4
        vals = E2M1[nib]
    vals = vals * np.repeat(np.exp2(scales.astype(np.float64) - 127.0), 8, axis=1)[..., None]
    return vals.transpose(0, 1, 3, 2).reshape(g * 512, n)


BS, N, D, B, D_PM = 2, 4096, 512, 8, 512


def sigmoid(v):
    return 1.0 / (1.0 + np.exp(-v))


def setup_inputs():
    k = mx_kscale(D)
    m = 3.0 * np.random.rand(BS, N, 1)
    H = bf(np.random.standard_normal((BS, N, D)) * k)
    surprise = bf(np.random.standard_normal((BS, N, D)) * m)
    w = np.random.standard_normal((D_PM, D)) / np.sqrt(D) / k
    words, scales = pack_weight(np.ascontiguousarray(w.T), "e4m3")
    return {"H": H,
            "surprise": surprise,
            "proj_in_w_words": words,
            "proj_in_w_scales": scales,
            "proj_in_b": bf(np.random.standard_normal(D_PM) * 0.1),
            "surp_scale": bf((1.0 + 0.1 * np.random.standard_normal(1)) / np.sqrt(D)),
            "surp_bias": bf(-1.5 + 0.1 * np.random.standard_normal(1))}


def reference(H, surprise, proj_in_w_words, proj_in_w_scales, proj_in_b, surp_scale, surp_bias):
    pre = (mxq(f64(H), 2, "e4m3") @ unpack_weight(proj_in_w_words, proj_in_w_scales, "e4m3")) + f64(proj_in_b)
    surp_mag = np.sqrt(np.sum(f64(surprise) ** 2, axis=-1))
    s = sigmoid(f64(surp_scale) * surp_mag + f64(surp_bias))
    weighted = np.sqrt(s)[..., None] * pre
    wq = mxq(weighted, 1, "e4m3")
    return (wq.transpose(0, 2, 1) @ wq) / N

@@ -1,0 +1,245 @@
+from contextlib import ExitStack
+
+import concourse.mybir as mybir
+from concourse.masks import make_identity
+
+F32 = mybir.dt.float32
+BF16 = mybir.dt.bfloat16
+I32 = mybir.dt.int32
+U32 = mybir.dt.uint32
+U8 = mybir.dt.uint8
+FP8X4 = mybir.dt.float8_e4m3fn_x4
+ALU = mybir.AluOpType
+ACT = mybir.ActivationFunctionType
+
+P = 128
+PACK = 4
+K_PASS = P * PACK
+SAMPLES = 2
+TOKENS = 4096
+D_IN = 512
+D_OUT = 512
+F_TILES = D_OUT // P
+GROUP = K_PASS
+T_TILES = GROUP // P
+GROUPS_PER_SAMPLE = TOKENS // GROUP
+GROUPS = SAMPLES * GROUPS_PER_SAMPLE
+
+FLOPS = 2 * SAMPLES * TOKENS * D_IN * D_OUT + 2 * SAMPLES * TOKENS * D_OUT * D_OUT
+
+
+def tile_proceduralmemory_pa_t_kernel(
+    tc, H, surprise, proj_in_w_words, proj_in_w_scales, proj_in_b, surp_scale, surp_bias, out
+):
+    nc = tc.nc
+    with ExitStack() as stack:
+        const = stack.enter_context(tc.tile_pool(name="const", bufs=1))
+        loads = stack.enter_context(tc.tile_pool(name="loads", bufs=GROUPS))
+        small = stack.enter_context(tc.tile_pool(name="small", bufs=6))
+        work = stack.enter_context(tc.tile_pool(name="work", bufs=3))
+        banks = stack.enter_context(tc.psum_pool(name="banks", bufs=4))
+        sums = stack.enter_context(tc.psum_pool(name="sums", bufs=1))
+        stack.enter_context(tc.manual_schedule())
+
+        w_scales = const.tile([P, D_OUT], U8, align_bytes=64)
+        nc.vector.memset(w_scales[:].bitcast(I32), 0)
+        for quadrant in range(4):
+            nc.sync.dma_start(
+                out=w_scales[32 * quadrant : 32 * quadrant + 4, :].bitcast(I32),
+                in_=proj_in_w_scales[0, 4 * quadrant : 4 * quadrant + 4, :].bitcast(I32),
+            )
+        w_codes = const.tile([P, D_OUT], U32, align_bytes=64)
+        nc.sync.dma_start(
+            out=w_codes[:].bitcast(I32),
+            in_=proj_in_w_words[0].rearrange("p n t -> p (n t)").bitcast(I32),
+        )
+
+        h_raw = {}
+        s_raw = {}
+        for g in range(GROUPS):
+            sample, first = g // GROUPS_PER_SAMPLE, (g % GROUPS_PER_SAMPLE) * GROUP
+            s_tile = loads.tile([P, T_TILES, D_IN], BF16, name="s_raw")
+            nc.sync.dma_start(
+                out=s_tile[:],
+                in_=surprise[sample, first : first + GROUP, :].rearrange("(p j) d -> p j d", j=T_TILES),
+            )
+            s_raw[g] = s_tile
+            h_tile = loads.tile([P, T_TILES, D_IN], BF16, name="h_raw")
+            nc.sync.dma_start(
+                out=h_tile[:],
+                in_=H[sample, first : first + GROUP, :].rearrange("(p j) d -> p j d", j=T_TILES),
+            )
+            h_raw[g] = h_tile
+
+        ident = const.tile([P, P], F32)
+        make_identity(nc, ident[:])
+        half = const.tile([P, T_TILES], F32)
+        nc.vector.memset(half[:], 0.5)
+        scale_bf = const.tile([P, 1], BF16)
+        nc.scalar.dma_start(out=scale_bf[:], in_=surp_scale.partition_broadcast(P))
+        bias_bf = const.tile([P, 1], BF16)
+        nc.scalar.dma_start(out=bias_bf[:], in_=surp_bias.partition_broadcast(P))
+        scale_col = const.tile([P, 1], F32)
+        nc.vector.tensor_copy(out=scale_col[:], in_=scale_bf[:])
+        bias_col = const.tile([P, 1], F32)
+        nc.vector.tensor_copy(out=bias_col[:], in_=bias_bf[:])
+        b_rows_bf = const.tile([P, P], BF16)
+        nc.vector.memset(b_rows_bf[:], 0.0)
+        nc.scalar.dma_start(out=b_rows_bf[0:F_TILES, :], in_=proj_in_b.rearrange("(m f) -> m f", f=P))
+        b_rows = const.tile([P, P], F32)
+        nc.vector.tensor_copy(out=b_rows[:], in_=b_rows_bf[:])
+        b_ps = banks.tile([P, P], F32, name="bank")
+        nc.tensor.transpose(out=b_ps[:], in_=b_rows[:], identity=ident[:])
+        b_col = const.tile([P, F_TILES], F32)
+        nc.vector.tensor_copy(out=b_col[:], in_=b_ps[:, 0:F_TILES])
+
+        mag = {}
+        root_gate = {}
+        gate_rows = {}
+        h_mx = {}
+        y_t = {}
+        y_grouped = {}
+        y_mx = {}
+        acc = {}
+
+        def squares(g):
+            junk = work.tile([P, T_TILES, D_IN], BF16, name="junk", bufs=2)
+            mag2 = small.tile([P, T_TILES], F32, name="mag2")
+            for j in range(T_TILES):
+                nc.scalar.activation(
+                    out=junk[:, j, :], in_=s_raw[g][:, j, :], func=ACT.Square, accum_out=mag2[:, j : j + 1]
+                )
+            mag_g = small.tile([P, T_TILES], F32, name="mag")
+            nc.gpsimd.tensor_tensor(out=mag_g[:], in0=mag2[:], in1=half[:], op=ALU.pow)
+            mag[g] = mag_g
+
+        def gate_finish(g):
+            gate = small.tile([P, T_TILES], F32, name="gate")
+            nc.scalar.activation(
+                out=gate[:], in_=mag[g][:], func=ACT.Sigmoid, bias=bias_col[:, 0:1], scale=scale_col[:, 0:1]
+            )
+            root = small.tile([P, T_TILES], F32, name="root")
+            nc.gpsimd.tensor_tensor(out=root[:], in0=gate[:], in1=half[:], op=ALU.pow)
+            root_gate[g] = root
+
+        def gate_spread(g):
+            spread_ps = banks.tile([P, T_TILES, P], F32, name="bank")
+            for j in range(T_TILES):
+                nc.tensor.transpose(
+                    out=spread_ps[:, j, :], in_=root_gate[g][:, j : j + 1].to_broadcast([P, P]), identity=ident[:]
+                )
+            rows = work.tile([P, GROUP], F32, name="gate_rows")
+            nc.scalar.copy(out=rows[:], in_=spread_ps[:].rearrange("p j n -> p (j n)"))
+            gate_rows[g] = rows
+
+        def h_transpose(g):
+            words = h_raw[g][:].bitcast(F32)
+            grouped = work.tile([P, PACK * GROUP], BF16, name="h_grouped", align_bytes=64, bufs=2)
+            grouped_words = grouped[:].bitcast(F32).rearrange("p (j n u) -> p j n u", j=T_TILES, u=2)
+            for pair in range(T_TILES // 2):
+                t_ps = banks.tile([P, 2, 2, P], F32, name="bank")
+                for jj in range(2):
+                    for u in range(2):
+                        nc.tensor.transpose(
+                            out=t_ps[:, jj, u, :], in_=words[:, 2 * pair + jj, u : D_IN // 2 : 2], identity=ident[:]
+                        )
+                nc.scalar.copy(
+                    out=grouped_words[:, 2 * pair : 2 * pair + 2], in_=t_ps[:].rearrange("p j u n -> p j n u")
+                )
+            return grouped
+
+        def quantise(grouped, name):
+            codes = work.tile([P, GROUP], U32, name=name + "_codes", align_bytes=64)
+            scales = work.tile([P, GROUP], U8, name=name + "_scales", align_bytes=64)
+            nc.vector.quantize_mx(out=codes[:].bitcast(FP8X4), scales=scales[:], in_=grouped[:])
+            return codes, scales
+
+        def project(g):
+            h_codes, h_scales = h_mx[g]
+            y_tile = work.tile([P, F_TILES, GROUP], BF16, name="y_t")
+            for m in range(F_TILES):
+                f_cols = slice(m * P, (m + 1) * P)
+                pre_ps = banks.tile([P, GROUP], F32, name="bank")
+                nc.tensor.matmul_mx(
+                    out=pre_ps[:],
+                    lhsT=w_codes[:, f_cols].bitcast(FP8X4),
+                    lhsT_scale=w_scales[:, f_cols],
+                    rhs=h_codes[:].bitcast(FP8X4),
+                    rhs_scale=h_scales[:],
+                    start=True,
+                    stop=True,
+                )
+                nc.vector.scalar_tensor_tensor(
+                    out=y_tile[:, m, :],
+                    in0=pre_ps[:],
+                    scalar=b_col[:, m : m + 1],
+                    in1=gate_rows[g][:],
+                    op0=ALU.add,
+                    op1=ALU.mult,
+                )
+            y_t[g] = y_tile
+
+        def y_transpose(g):
+            words = y_t[g][:].bitcast(F32)
+            grouped = work.tile([P, PACK * D_OUT], BF16, name="y_grouped", align_bytes=64, bufs=2)
+            grouped_words = grouped[:].bitcast(F32).rearrange("p (m f u) -> p m f u", m=F_TILES, u=2)
+            for pair in range(F_TILES // 2):
+                t_ps = banks.tile([P, 2, 2, P], F32, name="bank")
+                for mm in range(2):
+                    for u in range(2):
+                        nc.tensor.transpose(
+                            out=t_ps[:, mm, u, :], in_=words[:, 2 * pair + mm, u * P : (u + 1) * P], identity=ident[:]
+                        )
+                nc.vector.tensor_copy(
+                    out=grouped_words[:, 2 * pair : 2 * pair + 2], in_=t_ps[:].rearrange("p m u f -> p m f u")
+                )
+            return grouped
+
+        def gram(g):
+            sample, step = g // GROUPS_PER_SAMPLE, g % GROUPS_PER_SAMPLE
+            y_codes, y_scales = y_mx[g]
+            for m in range(F_TILES):
+                if step == 0:
+                    acc[m] = sums.tile([P, D_OUT], F32, name="acc%d" % m)
+                f_cols = slice(m * P, (m + 1) * P)
+                nc.tensor.matmul_mx(
+                    out=acc[m][:],
+                    lhsT=y_codes[:, f_cols].bitcast(FP8X4),
+                    lhsT_scale=y_scales[:, f_cols],
+                    rhs=y_codes[:].bitcast(FP8X4),
+                    rhs_scale=y_scales[:],
+                    start=(step == 0),
+                    stop=(step == GROUPS_PER_SAMPLE - 1),
+                )
+            if step == GROUPS_PER_SAMPLE - 1:
+                for m in range(F_TILES):
+                    g_rows = work.tile([P, D_OUT], F32, name="g_rows", bufs=4)
+                    if m % 2 == 0:
+                        nc.scalar.mul(out=g_rows[:], in_=acc[m][:], mul=1.0 / TOKENS)
+                    else:
+                        nc.vector.tensor_scalar_mul(out=g_rows[:], in0=acc[m][:], scalar1=1.0 / TOKENS)
+                    nc.sync.dma_start(out=out[sample, m * P : (m + 1) * P, :], in_=g_rows[:])
+
+        def live(g):
+            return 0 <= g < GROUPS
+
+        h_grouped = {}
+        for i in range(-3, GROUPS + 2):
+            if live(i + 1):
+                h_grouped[i + 1] = h_transpose(i + 1)
+            if live(i - 1):
+                y_grouped[i - 1] = y_transpose(i - 1)
+            if live(i + 1):
+                gate_spread(i + 1)
+            if live(i):
+                project(i)
+            if live(i - 2):
+                gram(i - 2)
+            if live(i + 1):
+                h_mx[i + 1] = quantise(h_grouped[i + 1], "h")
+            if live(i - 1):
+                y_mx[i - 1] = quantise(y_grouped[i - 1], "y")
+            if live(i + 2):
+                gate_finish(i + 2)
+            if live(i + 3):
+                squares(i + 3)

@@ -196,7 +196,7 @@ def tile_proceduralmemory_pa_t_kernel(
             return grouped
 
         def gram(g):
-            sample, step = g // GROUPS_PER_SAMPLE, g % GROUPS_PER_SAMPLE
+            step = g % GROUPS_PER_SAMPLE
             y_codes, y_scales = y_mx[g]
             for m in range(F_TILES):
                 if step == 0:
@@ -211,35 +211,38 @@ def tile_proceduralmemory_pa_t_kernel(
                     start=(step == 0),
                     stop=(step == GROUPS_PER_SAMPLE - 1),
                 )
-            if step == GROUPS_PER_SAMPLE - 1:
-                for m in range(F_TILES):
-                    g_rows = work.tile([P, D_OUT], F32, name="g_rows", bufs=4)
-                    if m % 2 == 0:
-                        nc.scalar.mul(out=g_rows[:], in_=acc[m][:], mul=1.0 / TOKENS)
-                    else:
-                        nc.vector.tensor_scalar_mul(out=g_rows[:], in0=acc[m][:], scalar1=1.0 / TOKENS)
-                    nc.sync.dma_start(out=out[sample, m * P : (m + 1) * P, :], in_=g_rows[:])
+
+        def finish(sample):
+            for m in range(F_TILES):
+                g_rows = work.tile([P, D_OUT], F32, name="g_rows", bufs=4)
+                if m % 2 == 0:
+                    nc.scalar.mul(out=g_rows[:], in_=acc[m][:], mul=1.0 / TOKENS)
+                else:
+                    nc.vector.tensor_scalar_mul(out=g_rows[:], in0=acc[m][:], scalar1=1.0 / TOKENS)
+                nc.sync.dma_start(out=out[sample, m * P : (m + 1) * P, :], in_=g_rows[:])
 
         def live(g):
             return 0 <= g < GROUPS
 
         h_grouped = {}
-        for i in range(-3, GROUPS + 2):
+        for i in range(-2, GROUPS + 2):
+            if live(i):
+                gate_spread(i)
             if live(i + 1):
                 h_grouped[i + 1] = h_transpose(i + 1)
-            if live(i - 1):
-                y_grouped[i - 1] = y_transpose(i - 1)
-            if live(i + 1):
-                gate_spread(i + 1)
             if live(i):
                 project(i)
+            if live(i - 1):
+                y_grouped[i - 1] = y_transpose(i - 1)
             if live(i - 2):
                 gram(i - 2)
             if live(i + 1):
                 h_mx[i + 1] = quantise(h_grouped[i + 1], "h")
             if live(i - 1):
                 y_mx[i - 1] = quantise(y_grouped[i - 1], "y")
+            if live(i + 1):
+                gate_finish(i + 1)
             if live(i + 2):
-                gate_finish(i + 2)
-            if live(i + 3):
-                squares(i + 3)
+                squares(i + 2)
+            if live(i - 2) and (i - 2) % GROUPS_PER_SAMPLE == GROUPS_PER_SAMPLE - 1:
+                finish((i - 2) // GROUPS_PER_SAMPLE)

@@ -83,15 +83,8 @@ def tile_proceduralmemory_pa_t_kernel(
         nc.vector.tensor_copy(out=scale_col[:], in_=scale_bf[:])
         bias_col = const.tile([P, 1], F32)
         nc.vector.tensor_copy(out=bias_col[:], in_=bias_bf[:])
-        b_rows_bf = const.tile([P, P], BF16)
-        nc.vector.memset(b_rows_bf[:], 0.0)
-        nc.scalar.dma_start(out=b_rows_bf[0:F_TILES, :], in_=proj_in_b.rearrange("(m f) -> m f", f=P))
-        b_rows = const.tile([P, P], F32)
-        nc.vector.tensor_copy(out=b_rows[:], in_=b_rows_bf[:])
-        b_ps = banks.tile([P, P], F32, name="bank")
-        nc.tensor.transpose(out=b_ps[:], in_=b_rows[:], identity=ident[:])
-        b_col = const.tile([P, F_TILES], F32)
-        nc.vector.tensor_copy(out=b_col[:], in_=b_ps[:, 0:F_TILES])
+        b_rows = const.tile([P, D_OUT], BF16)
+        nc.scalar.dma_start(out=b_rows[:], in_=proj_in_b.partition_broadcast(P))
 
         mag = {}
         root_gate = {}
@@ -122,14 +115,13 @@ def tile_proceduralmemory_pa_t_kernel(
             nc.gpsimd.tensor_tensor(out=root[:], in0=gate[:], in1=half[:], op=ALU.pow)
             root_gate[g] = root
 
-        def gate_spread(g):
-            spread_ps = banks.tile([P, T_TILES, P], F32, name="bank")
+        def bias_rows(g):
+            rows = work.tile([P, T_TILES, D_OUT], F32, name="gated_bias", bufs=2)
             for j in range(T_TILES):
-                nc.tensor.transpose(
-                    out=spread_ps[:, j, :], in_=root_gate[g][:, j : j + 1].to_broadcast([P, P]), identity=ident[:]
-                )
-            rows = work.tile([P, GROUP], F32, name="gate_rows")
-            nc.scalar.copy(out=rows[:], in_=spread_ps[:].rearrange("p j n -> p (j n)"))
+                if j % 2 == 0:
+                    nc.vector.tensor_scalar_mul(out=rows[:, j, :], in0=b_rows[:], scalar1=root_gate[g][:, j : j + 1])
+                else:
+                    nc.scalar.mul(out=rows[:, j, :], in_=b_rows[:], mul=root_gate[g][:, j : j + 1])
             gate_rows[g] = rows
 
         def h_transpose(g):
@@ -151,48 +143,40 @@ def tile_proceduralmemory_pa_t_kernel(
         def quantise(grouped, name):
             codes = work.tile([P, GROUP], U32, name=name + "_codes", align_bytes=64)
             scales = work.tile([P, GROUP], U8, name=name + "_scales", align_bytes=64)
-            nc.vector.quantize_mx(out=codes[:].bitcast(FP8X4), scales=scales[:], in_=grouped[:])
+            nc.vector.quantize_mx(out=codes[:].bitcast(FP8X4), scales=scales[:], in_=grouped)
             return codes, scales
 
         def project(g):
             h_codes, h_scales = h_mx[g]
-            y_tile = work.tile([P, F_TILES, GROUP], BF16, name="y_t")
-            for m in range(F_TILES):
-                f_cols = slice(m * P, (m + 1) * P)
-                pre_ps = banks.tile([P, GROUP], F32, name="bank")
+            y_tile = work.tile([P, T_TILES, D_OUT], BF16, name="y_t", bufs=2)
+            for j in range(T_TILES):
+                t_cols = slice(j * P, (j + 1) * P)
+                pre_ps = banks.tile([P, D_OUT], F32, name="bank")
                 nc.tensor.matmul_mx(
                     out=pre_ps[:],
-                    lhsT=w_codes[:, f_cols].bitcast(FP8X4),
-                    lhsT_scale=w_scales[:, f_cols],
-                    rhs=h_codes[:].bitcast(FP8X4),
-                    rhs_scale=h_scales[:],
+                    lhsT=h_codes[:, t_cols].bitcast(FP8X4),
+                    lhsT_scale=h_scales[:, t_cols],
+                    rhs=w_codes[:].bitcast(FP8X4),
+                    rhs_scale=w_scales[:],
                     start=True,
                     stop=True,
                 )
                 nc.vector.scalar_tensor_tensor(
-                    out=y_tile[:, m, :],
+                    out=y_tile[:, j, :],
                     in0=pre_ps[:],
-                    scalar=b_col[:, m : m + 1],
-                    in1=gate_rows[g][:],
-                    op0=ALU.add,
-                    op1=ALU.mult,
+                    scalar=root_gate[g][:, j : j + 1],
+                    in1=gate_rows[g][:, j, :],
+                    op0=ALU.mult,
+                    op1=ALU.add,
                 )
             y_t[g] = y_tile
 
-        def y_transpose(g):
-            words = y_t[g][:].bitcast(F32)
-            grouped = work.tile([P, PACK * D_OUT], BF16, name="y_grouped", align_bytes=64, bufs=2)
-            grouped_words = grouped[:].bitcast(F32).rearrange("p (m f u) -> p m f u", m=F_TILES, u=2)
-            for pair in range(F_TILES // 2):
-                t_ps = banks.tile([P, 2, 2, P], F32, name="bank")
-                for mm in range(2):
-                    for u in range(2):
-                        nc.tensor.transpose(
-                            out=t_ps[:, mm, u, :], in_=words[:, 2 * pair + mm, u * P : (u + 1) * P], identity=ident[:]
-                        )
-                nc.vector.tensor_copy(
-                    out=grouped_words[:, 2 * pair : 2 * pair + 2], in_=t_ps[:].rearrange("p m u f -> p m f u")
-                )
+        def regroup(g):
+            grouped = work.tile([P, D_OUT, PACK], BF16, name="y_grouped", align_bytes=64, bufs=2)
+            nc.vector.tensor_copy(
+                out=grouped[:].rearrange("p (c i) j -> p c j i", i=4),
+                in_=y_t[g][:].rearrange("p j (c i) -> p c j i", i=4),
+            )
             return grouped
 
         def gram(g):
@@ -225,24 +209,23 @@ def tile_proceduralmemory_pa_t_kernel(
             return 0 <= g < GROUPS
 
         h_grouped = {}
-        for i in range(-2, GROUPS + 2):
-            if live(i):
-                gate_spread(i)
+        for i in range(-2, GROUPS + 1):
             if live(i + 1):
+                gate_finish(i + 1)
                 h_grouped[i + 1] = h_transpose(i + 1)
             if live(i):
                 project(i)
             if live(i - 1):
-                y_grouped[i - 1] = y_transpose(i - 1)
-            if live(i - 2):
-                gram(i - 2)
+                gram(i - 1)
             if live(i + 1):
-                h_mx[i + 1] = quantise(h_grouped[i + 1], "h")
-            if live(i - 1):
-                y_mx[i - 1] = quantise(y_grouped[i - 1], "y")
-            if live(i + 1):
-                gate_finish(i + 1)
+                h_mx[i + 1] = quantise(h_grouped[i + 1][:], "h")
+            if live(i):
+                y_grouped[i] = regroup(i)
             if live(i + 2):
                 squares(i + 2)
-            if live(i - 2) and (i - 2) % GROUPS_PER_SAMPLE == GROUPS_PER_SAMPLE - 1:
-                finish((i - 2) // GROUPS_PER_SAMPLE)
+            if live(i + 1):
+                bias_rows(i + 1)
+            if live(i):
+                y_mx[i] = quantise(y_grouped[i][:].rearrange("p f j -> p (f j)"), "y")
+            if live(i - 1) and (i - 1) % GROUPS_PER_SAMPLE == GROUPS_PER_SAMPLE - 1:
+                finish((i - 1) // GROUPS_PER_SAMPLE)

@@ -83,8 +83,15 @@ def tile_proceduralmemory_pa_t_kernel(
         nc.vector.tensor_copy(out=scale_col[:], in_=scale_bf[:])
         bias_col = const.tile([P, 1], F32)
         nc.vector.tensor_copy(out=bias_col[:], in_=bias_bf[:])
-        b_rows = const.tile([P, D_OUT], BF16)
-        nc.scalar.dma_start(out=b_rows[:], in_=proj_in_b.partition_broadcast(P))
+        b_rows_bf = const.tile([P, P], BF16)
+        nc.vector.memset(b_rows_bf[:], 0.0)
+        nc.scalar.dma_start(out=b_rows_bf[0:F_TILES, :], in_=proj_in_b.rearrange("(m f) -> m f", f=P))
+        b_rows = const.tile([P, P], F32)
+        nc.vector.tensor_copy(out=b_rows[:], in_=b_rows_bf[:])
+        b_ps = banks.tile([P, P], F32, name="bank")
+        nc.tensor.transpose(out=b_ps[:], in_=b_rows[:], identity=ident[:])
+        b_col = const.tile([P, F_TILES], F32)
+        nc.vector.tensor_copy(out=b_col[:], in_=b_ps[:, 0:F_TILES])
 
         mag = {}
         root_gate = {}
@@ -115,13 +122,14 @@ def tile_proceduralmemory_pa_t_kernel(
             nc.gpsimd.tensor_tensor(out=root[:], in0=gate[:], in1=half[:], op=ALU.pow)
             root_gate[g] = root
 
-        def bias_rows(g):
-            rows = work.tile([P, T_TILES, D_OUT], F32, name="gated_bias", bufs=2)
+        def gate_spread(g):
+            spread_ps = banks.tile([P, T_TILES, P], F32, name="bank")
             for j in range(T_TILES):
-                if j % 2 == 0:
-                    nc.vector.tensor_scalar_mul(out=rows[:, j, :], in0=b_rows[:], scalar1=root_gate[g][:, j : j + 1])
-                else:
-                    nc.scalar.mul(out=rows[:, j, :], in_=b_rows[:], mul=root_gate[g][:, j : j + 1])
+                nc.tensor.transpose(
+                    out=spread_ps[:, j, :], in_=root_gate[g][:, j : j + 1].to_broadcast([P, P]), identity=ident[:]
+                )
+            rows = work.tile([P, GROUP], F32, name="gate_rows")
+            nc.scalar.copy(out=rows[:], in_=spread_ps[:].rearrange("p j n -> p (j n)"))
             gate_rows[g] = rows
 
         def h_transpose(g):
@@ -143,40 +151,47 @@ def tile_proceduralmemory_pa_t_kernel(
         def quantise(grouped, name):
             codes = work.tile([P, GROUP], U32, name=name + "_codes", align_bytes=64)
             scales = work.tile([P, GROUP], U8, name=name + "_scales", align_bytes=64)
-            nc.vector.quantize_mx(out=codes[:].bitcast(FP8X4), scales=scales[:], in_=grouped)
+            nc.vector.quantize_mx(out=codes[:].bitcast(FP8X4), scales=scales[:], in_=grouped[:])
             return codes, scales
 
         def project(g):
             h_codes, h_scales = h_mx[g]
-            y_tile = work.tile([P, T_TILES, D_OUT], BF16, name="y_t", bufs=2)
-            for j in range(T_TILES):
-                t_cols = slice(j * P, (j + 1) * P)
-                pre_ps = banks.tile([P, D_OUT], F32, name="bank")
+            y_tile = work.tile([P, F_TILES, GROUP], BF16, name="y_t")
+            for m in range(F_TILES):
+                f_cols = slice(m * P, (m + 1) * P)
+                pre_ps = banks.tile([P, GROUP], F32, name="bank")
                 nc.tensor.matmul_mx(
                     out=pre_ps[:],
-                    lhsT=h_codes[:, t_cols].bitcast(FP8X4),
-                    lhsT_scale=h_scales[:, t_cols],
-                    rhs=w_codes[:].bitcast(FP8X4),
-                    rhs_scale=w_scales[:],
+                    lhsT=w_codes[:, f_cols].bitcast(FP8X4),
+                    lhsT_scale=w_scales[:, f_cols],
+                    rhs=h_codes[:].bitcast(FP8X4),
+                    rhs_scale=h_scales[:],
                     start=True,
                     stop=True,
                 )
                 nc.vector.scalar_tensor_tensor(
-                    out=y_tile[:, j, :],
+                    out=y_tile[:, m, :],
                     in0=pre_ps[:],
-                    scalar=root_gate[g][:, j : j + 1],
-                    in1=gate_rows[g][:, j, :],
-                    op0=ALU.mult,
-                    op1=ALU.add,
+                    scalar=b_col[:, m : m + 1],
+                    in1=gate_rows[g][:],
+                    op0=ALU.add,
+                    op1=ALU.mult,
                 )
             y_t[g] = y_tile
 
-        def regroup(g):
-            grouped = work.tile([P, D_OUT, PACK], BF16, name="y_grouped", align_bytes=64, bufs=2)
-            nc.vector.tensor_copy(
-                out=grouped[:].rearrange("p (c i) j -> p c j i", i=4),
-                in_=y_t[g][:].rearrange("p j (c i) -> p c j i", i=4),
-            )
+        def y_transpose(g):
+            words = y_t[g][:].bitcast(F32)
+            grouped = work.tile([P, PACK * D_OUT], BF16, name="y_grouped", align_bytes=64, bufs=2)
+            grouped_words = grouped[:].bitcast(F32).rearrange("p (m f u) -> p m f u", m=F_TILES, u=2)
+            for pair in range(F_TILES // 2):
+                t_ps = banks.tile([P, 2, 2, P], F32, name="bank")
+                for mm in range(2):
+                    for u in range(2):
+                        nc.tensor.transpose(
+                            out=t_ps[:, mm, u, :], in_=words[:, 2 * pair + mm, u * P : (u + 1) * P], identity=ident[:]
+                        )
+                copy_out = nc.vector.tensor_copy if pair == 0 else nc.scalar.copy
+                copy_out(out=grouped_words[:, 2 * pair : 2 * pair + 2], in_=t_ps[:].rearrange("p m u f -> p m f u"))
             return grouped
 
         def gram(g):
@@ -209,23 +224,24 @@ def tile_proceduralmemory_pa_t_kernel(
             return 0 <= g < GROUPS
 
         h_grouped = {}
-        for i in range(-2, GROUPS + 1):
+        for i in range(-2, GROUPS + 2):
             if live(i + 1):
-                gate_finish(i + 1)
                 h_grouped[i + 1] = h_transpose(i + 1)
             if live(i):
-                project(i)
+                gate_spread(i)
             if live(i - 1):
-                gram(i - 1)
-            if live(i + 1):
-                h_mx[i + 1] = quantise(h_grouped[i + 1][:], "h")
+                y_grouped[i - 1] = y_transpose(i - 1)
             if live(i):
-                y_grouped[i] = regroup(i)
+                project(i)
+            if live(i - 2):
+                gram(i - 2)
+            if live(i + 1):
+                h_mx[i + 1] = quantise(h_grouped[i + 1], "h")
+            if live(i - 1):
+                y_mx[i - 1] = quantise(y_grouped[i - 1], "y")
+            if live(i + 1):
+                gate_finish(i + 1)
             if live(i + 2):
                 squares(i + 2)
-            if live(i + 1):
-                bias_rows(i + 1)
-            if live(i):
-                y_mx[i] = quantise(y_grouped[i][:].rearrange("p f j -> p (f j)"), "y")
-            if live(i - 1) and (i - 1) % GROUPS_PER_SAMPLE == GROUPS_PER_SAMPLE - 1:
-                finish((i - 1) // GROUPS_PER_SAMPLE)
+            if live(i - 2) and (i - 2) % GROUPS_PER_SAMPLE == GROUPS_PER_SAMPLE - 1:
+                finish((i - 2) // GROUPS_PER_SAMPLE)

@@ -24,6 +24,7 @@ GROUP = K_PASS
 T_TILES = GROUP // P
 GROUPS_PER_SAMPLE = TOKENS // GROUP
 GROUPS = SAMPLES * GROUPS_PER_SAMPLE
+MX_WIDTHS = (128, 256, 512)
 
 FLOPS = 2 * SAMPLES * TOKENS * D_IN * D_OUT + 2 * SAMPLES * TOKENS * D_OUT * D_OUT
 
@@ -75,23 +76,23 @@ def tile_proceduralmemory_pa_t_kernel(
         make_identity(nc, ident[:])
         half = const.tile([P, T_TILES], F32)
         nc.vector.memset(half[:], 0.5)
+        b_rows_bf = const.tile([P, P], BF16)
+        nc.vector.memset(b_rows_bf[:], 0.0)
+        nc.scalar.dma_start(out=b_rows_bf[0:F_TILES, :], in_=proj_in_b.rearrange("(m f) -> m f", f=P))
         scale_bf = const.tile([P, 1], BF16)
         nc.scalar.dma_start(out=scale_bf[:], in_=surp_scale.partition_broadcast(P))
         bias_bf = const.tile([P, 1], BF16)
         nc.scalar.dma_start(out=bias_bf[:], in_=surp_bias.partition_broadcast(P))
-        scale_col = const.tile([P, 1], F32)
-        nc.vector.tensor_copy(out=scale_col[:], in_=scale_bf[:])
-        bias_col = const.tile([P, 1], F32)
-        nc.vector.tensor_copy(out=bias_col[:], in_=bias_bf[:])
-        b_rows_bf = const.tile([P, P], BF16)
-        nc.vector.memset(b_rows_bf[:], 0.0)
-        nc.scalar.dma_start(out=b_rows_bf[0:F_TILES, :], in_=proj_in_b.rearrange("(m f) -> m f", f=P))
         b_rows = const.tile([P, P], F32)
         nc.vector.tensor_copy(out=b_rows[:], in_=b_rows_bf[:])
         b_ps = banks.tile([P, P], F32, name="bank")
         nc.tensor.transpose(out=b_ps[:], in_=b_rows[:], identity=ident[:])
         b_col = const.tile([P, F_TILES], F32)
         nc.vector.tensor_copy(out=b_col[:], in_=b_ps[:, 0:F_TILES])
+        scale_col = const.tile([P, 1], F32)
+        nc.vector.tensor_copy(out=scale_col[:], in_=scale_bf[:])
+        bias_col = const.tile([P, 1], F32)
+        nc.vector.tensor_copy(out=bias_col[:], in_=bias_bf[:])
 
         mag = {}
         root_gate = {}
@@ -101,6 +102,7 @@ def tile_proceduralmemory_pa_t_kernel(
         y_grouped = {}
         y_mx = {}
         acc = {}
+        g_rows = {}
 
         def squares(g):
             junk = work.tile([P, T_TILES, D_IN], BF16, name="junk", bufs=2)
@@ -149,35 +151,34 @@ def tile_proceduralmemory_pa_t_kernel(
             return grouped
 
         def quantise(grouped, name):
-            codes = work.tile([P, GROUP], U32, name=name + "_codes", align_bytes=64)
-            scales = work.tile([P, GROUP], U8, name=name + "_scales", align_bytes=64)
+            codes = work.tile([P, GROUP], U32, name=name + "_codes", align_bytes=64, bufs=4)
+            scales = work.tile([P, GROUP], U8, name=name + "_scales", align_bytes=64, bufs=4)
             nc.vector.quantize_mx(out=codes[:].bitcast(FP8X4), scales=scales[:], in_=grouped[:])
             return codes, scales
 
-        def project(g):
+        def project_pass(g, m):
             h_codes, h_scales = h_mx[g]
-            y_tile = work.tile([P, F_TILES, GROUP], BF16, name="y_t")
-            for m in range(F_TILES):
-                f_cols = slice(m * P, (m + 1) * P)
-                pre_ps = banks.tile([P, GROUP], F32, name="bank")
-                nc.tensor.matmul_mx(
-                    out=pre_ps[:],
-                    lhsT=w_codes[:, f_cols].bitcast(FP8X4),
-                    lhsT_scale=w_scales[:, f_cols],
-                    rhs=h_codes[:].bitcast(FP8X4),
-                    rhs_scale=h_scales[:],
-                    start=True,
-                    stop=True,
-                )
-                nc.vector.scalar_tensor_tensor(
-                    out=y_tile[:, m, :],
-                    in0=pre_ps[:],
-                    scalar=b_col[:, m : m + 1],
-                    in1=gate_rows[g][:],
-                    op0=ALU.add,
-                    op1=ALU.mult,
-                )
-            y_t[g] = y_tile
+            if m == 0:
+                y_t[g] = work.tile([P, F_TILES, GROUP], BF16, name="y_t")
+            f_cols = slice(m * P, (m + 1) * P)
+            pre_ps = banks.tile([P, GROUP], F32, name="bank")
+            nc.tensor.matmul_mx(
+                out=pre_ps[:],
+                lhsT=w_codes[:, f_cols].bitcast(FP8X4),
+                lhsT_scale=w_scales[:, f_cols],
+                rhs=h_codes[:].bitcast(FP8X4),
+                rhs_scale=h_scales[:],
+                start=True,
+                stop=True,
+            )
+            nc.vector.scalar_tensor_tensor(
+                out=y_t[g][:, m, :],
+                in0=pre_ps[:],
+                scalar=b_col[:, m : m + 1],
+                in1=gate_rows[g][:],
+                op0=ALU.add,
+                op1=ALU.mult,
+            )
 
         def y_transpose(g):
             words = y_t[g][:].bitcast(F32)
@@ -194,54 +195,77 @@ def tile_proceduralmemory_pa_t_kernel(
                 copy_out(out=grouped_words[:, 2 * pair : 2 * pair + 2], in_=t_ps[:].rearrange("p m u f -> p m f u"))
             return grouped
 
-        def gram(g):
+        def gram_width(m):
+            return min(w for w in MX_WIDTHS if w >= D_OUT - m * P)
+
+        def gram_pass(g, m):
             step = g % GROUPS_PER_SAMPLE
             y_codes, y_scales = y_mx[g]
-            for m in range(F_TILES):
-                if step == 0:
-                    acc[m] = sums.tile([P, D_OUT], F32, name="acc%d" % m)
-                f_cols = slice(m * P, (m + 1) * P)
-                nc.tensor.matmul_mx(
-                    out=acc[m][:],
-                    lhsT=y_codes[:, f_cols].bitcast(FP8X4),
-                    lhsT_scale=y_scales[:, f_cols],
-                    rhs=y_codes[:].bitcast(FP8X4),
-                    rhs_scale=y_scales[:],
-                    start=(step == 0),
-                    stop=(step == GROUPS_PER_SAMPLE - 1),
-                )
+            if step == 0:
+                acc[m] = sums.tile([P, gram_width(m)], F32, name="acc%d" % m)
+            f_cols = slice(m * P, (m + 1) * P)
+            right = slice(D_OUT - gram_width(m), D_OUT)
+            nc.tensor.matmul_mx(
+                out=acc[m][:],
+                lhsT=y_codes[:, f_cols].bitcast(FP8X4),
+                lhsT_scale=y_scales[:, f_cols],
+                rhs=y_codes[:, right].bitcast(FP8X4),
+                rhs_scale=y_scales[:, right],
+                start=(step == 0),
+                stop=(step == GROUPS_PER_SAMPLE - 1),
+            )
 
-        def finish(sample):
+        def drain():
             for m in range(F_TILES):
-                g_rows = work.tile([P, D_OUT], F32, name="g_rows", bufs=4)
+                g_rows[m] = work.tile([P, D_OUT], F32, name="g_rows", bufs=F_TILES)
+                right = g_rows[m][:, D_OUT - gram_width(m) : D_OUT]
                 if m % 2 == 0:
-                    nc.scalar.mul(out=g_rows[:], in_=acc[m][:], mul=1.0 / TOKENS)
+                    nc.scalar.mul(out=right, in_=acc[m][:], mul=1.0 / TOKENS)
                 else:
-                    nc.vector.tensor_scalar_mul(out=g_rows[:], in0=acc[m][:], scalar1=1.0 / TOKENS)
-                nc.sync.dma_start(out=out[sample, m * P : (m + 1) * P, :], in_=g_rows[:])
+                    nc.vector.tensor_scalar_mul(out=right, in0=acc[m][:], scalar1=1.0 / TOKENS)
+
+        def mirror_and_store(sample):
+            for m in range(F_TILES):
+                missing = (D_OUT - gram_width(m)) // P
+                if missing > 0:
+                    mirror_ps = banks.tile([P, missing, P], F32, name="bank")
+                    for n in range(missing):
+                        nc.tensor.transpose(
+                            out=mirror_ps[:, n, :], in_=g_rows[n][:, m * P : (m + 1) * P], identity=ident[:]
+                        )
+                    nc.scalar.copy(
+                        out=g_rows[m][:, 0 : missing * P], in_=mirror_ps[:].rearrange("p n f -> p (n f)")
+                    )
+                nc.sync.dma_start(out=out[sample, m * P : (m + 1) * P, :], in_=g_rows[m][:])
 
         def live(g):
             return 0 <= g < GROUPS
 
+        def last_of_sample(g):
+            return live(g) and g % GROUPS_PER_SAMPLE == GROUPS_PER_SAMPLE - 1
+
         h_grouped = {}
-        for i in range(-2, GROUPS + 2):
-            if live(i + 1):
-                h_grouped[i + 1] = h_transpose(i + 1)
+        for i in range(-2, GROUPS + 3):
+            if live(i + 2):
+                h_grouped[i + 2] = h_transpose(i + 2)
             if live(i):
                 gate_spread(i)
             if live(i - 1):
                 y_grouped[i - 1] = y_transpose(i - 1)
-            if live(i):
-                project(i)
-            if live(i - 2):
-                gram(i - 2)
-            if live(i + 1):
-                h_mx[i + 1] = quantise(h_grouped[i + 1], "h")
+            if last_of_sample(i - 3):
+                mirror_and_store((i - 3) // GROUPS_PER_SAMPLE)
+            for m in range(F_TILES):
+                if live(i):
+                    project_pass(i, m)
+                if live(i - 2):
+                    gram_pass(i - 2, m)
+            if live(i + 2):
+                h_mx[i + 2] = quantise(h_grouped[i + 2], "h")
             if live(i - 1):
                 y_mx[i - 1] = quantise(y_grouped[i - 1], "y")
             if live(i + 1):
                 gate_finish(i + 1)
             if live(i + 2):
                 squares(i + 2)
-            if live(i - 2) and (i - 2) % GROUPS_PER_SAMPLE == GROUPS_PER_SAMPLE - 1:
-                finish((i - 2) // GROUPS_PER_SAMPLE)
+            if last_of_sample(i - 2):
+                drain()

@@ -74,7 +74,7 @@ def tile_proceduralmemory_pa_t_kernel(
 
         ident = const.tile([P, P], F32)
         make_identity(nc, ident[:])
-        half = const.tile([P, T_TILES], F32)
+        half = const.tile([P, 2, T_TILES], F32)
         nc.vector.memset(half[:], 0.5)
         b_rows_bf = const.tile([P, P], BF16)
         nc.vector.memset(b_rows_bf[:], 0.0)
@@ -104,25 +104,30 @@ def tile_proceduralmemory_pa_t_kernel(
         acc = {}
         g_rows = {}
 
-        def squares(g):
-            junk = work.tile([P, T_TILES, D_IN], BF16, name="junk", bufs=2)
-            mag2 = small.tile([P, T_TILES], F32, name="mag2")
-            for j in range(T_TILES):
+        def gate_step(g_new, g_old):
+            radicands = small.tile([P, 2, T_TILES], F32, name="radicands")
+            roots = small.tile([P, 2, T_TILES], F32, name="roots")
+            if live(g_new):
+                junk = work.tile([P, T_TILES, D_IN], BF16, name="junk", bufs=2)
+                for j in range(T_TILES):
+                    nc.scalar.activation(
+                        out=junk[:, j, :],
+                        in_=s_raw[g_new][:, j, :],
+                        func=ACT.Square,
+                        accum_out=radicands[:, 0, j : j + 1],
+                    )
+            if live(g_old):
                 nc.scalar.activation(
-                    out=junk[:, j, :], in_=s_raw[g][:, j, :], func=ACT.Square, accum_out=mag2[:, j : j + 1]
+                    out=radicands[:, 1, :],
+                    in_=mag[g_old],
+                    func=ACT.Sigmoid,
+                    bias=bias_col[:, 0:1],
+                    scale=scale_col[:, 0:1],
                 )
-            mag_g = small.tile([P, T_TILES], F32, name="mag")
-            nc.gpsimd.tensor_tensor(out=mag_g[:], in0=mag2[:], in1=half[:], op=ALU.pow)
-            mag[g] = mag_g
-
-        def gate_finish(g):
-            gate = small.tile([P, T_TILES], F32, name="gate")
-            nc.scalar.activation(
-                out=gate[:], in_=mag[g][:], func=ACT.Sigmoid, bias=bias_col[:, 0:1], scale=scale_col[:, 0:1]
-            )
-            root = small.tile([P, T_TILES], F32, name="root")
-            nc.gpsimd.tensor_tensor(out=root[:], in0=gate[:], in1=half[:], op=ALU.pow)
-            root_gate[g] = root
+            rows = slice(0 if live(g_new) else 1, 2 if live(g_old) else 1)
+            nc.gpsimd.tensor_tensor(out=roots[:, rows, :], in0=radicands[:, rows, :], in1=half[:, rows, :], op=ALU.pow)
+            mag[g_new] = roots[:, 0, :]
+            root_gate[g_old] = roots[:, 1, :]
 
         def gate_spread(g):
             spread_ps = banks.tile([P, T_TILES, P], F32, name="bank")
@@ -245,7 +250,7 @@ def tile_proceduralmemory_pa_t_kernel(
             return live(g) and g % GROUPS_PER_SAMPLE == GROUPS_PER_SAMPLE - 1
 
         h_grouped = {}
-        for i in range(-2, GROUPS + 3):
+        for i in range(-3, GROUPS + 3):
             if live(i + 2):
                 h_grouped[i + 2] = h_transpose(i + 2)
             if live(i):
@@ -263,9 +268,7 @@ def tile_proceduralmemory_pa_t_kernel(
                 h_mx[i + 2] = quantise(h_grouped[i + 2], "h")
             if live(i - 1):
                 y_mx[i - 1] = quantise(y_grouped[i - 1], "y")
-            if live(i + 1):
-                gate_finish(i + 1)
-            if live(i + 2):
-                squares(i + 2)
+            if live(i + 3) or live(i + 2):
+                gate_step(i + 3, i + 2)
             if last_of_sample(i - 2):
                 drain()

@@ -28,6 +28,21 @@ MX_WIDTHS = (128, 256, 512)
 
 FLOPS = 2 * SAMPLES * TOKENS * D_IN * D_OUT + 2 * SAMPLES * TOKENS * D_OUT * D_OUT
 
+LEAD = 2
+GATE_LAG = 2
+
+
+def spread_engine(g):
+    return "V" if g < 1 else "S"
+
+
+def h_engine(g, pair):
+    return "V" if g < 2 or (pair == 1 and g % 2 == 1) else "S"
+
+
+def y_engine(g, pair):
+    return "V" if pair == 0 else "S"
+
 
 def tile_proceduralmemory_pa_t_kernel(
     tc, H, surprise, proj_in_w_words, proj_in_w_scales, proj_in_b, surp_scale, surp_bias, out
@@ -36,12 +51,30 @@ def tile_proceduralmemory_pa_t_kernel(
     with ExitStack() as stack:
         const = stack.enter_context(tc.tile_pool(name="const", bufs=1))
         loads = stack.enter_context(tc.tile_pool(name="loads", bufs=GROUPS))
-        small = stack.enter_context(tc.tile_pool(name="small", bufs=6))
+        small = stack.enter_context(tc.tile_pool(name="small", bufs=8))
         work = stack.enter_context(tc.tile_pool(name="work", bufs=3))
         banks = stack.enter_context(tc.psum_pool(name="banks", bufs=4))
         sums = stack.enter_context(tc.psum_pool(name="sums", bufs=1))
         stack.enter_context(tc.manual_schedule())
 
+
+        h_raw = {}
+        s_raw = {}
+
+        def tokens_of(array, g):
+            sample, first = g // GROUPS_PER_SAMPLE, (g % GROUPS_PER_SAMPLE) * GROUP
+            return array[sample, first : first + GROUP, :].rearrange("(p j) d -> p j d", j=T_TILES)
+
+        def load(array, g, kept, name, parts):
+            tile = loads.tile([P, T_TILES, D_IN], BF16, name=name)
+            step = T_TILES // parts
+            for j in range(0, T_TILES, step):
+                nc.sync.dma_start(out=tile[:, j : j + step, :], in_=tokens_of(array, g)[:, j : j + step, :])
+            kept[g] = tile
+
+        load(surprise, 0, s_raw, "s_raw", 2)
+        load(H, 0, h_raw, "h_raw", 1)
+        load(surprise, 1, s_raw, "s_raw", 1)
         w_scales = const.tile([P, D_OUT], U8, align_bytes=64)
         nc.vector.memset(w_scales[:].bitcast(I32), 0)
         for quadrant in range(4):
@@ -54,47 +87,38 @@ def tile_proceduralmemory_pa_t_kernel(
             out=w_codes[:].bitcast(I32),
             in_=proj_in_w_words[0].rearrange("p n t -> p (n t)").bitcast(I32),
         )
+        load(H, 1, h_raw, "h_raw", 1)
+        for g in range(2, GROUPS):
+            load(surprise, g, s_raw, "s_raw", 1)
+            load(H, g, h_raw, "h_raw", 1)
 
-        h_raw = {}
-        s_raw = {}
-        for g in range(GROUPS):
-            sample, first = g // GROUPS_PER_SAMPLE, (g % GROUPS_PER_SAMPLE) * GROUP
-            s_tile = loads.tile([P, T_TILES, D_IN], BF16, name="s_raw")
-            nc.sync.dma_start(
-                out=s_tile[:],
-                in_=surprise[sample, first : first + GROUP, :].rearrange("(p j) d -> p j d", j=T_TILES),
-            )
-            s_raw[g] = s_tile
-            h_tile = loads.tile([P, T_TILES, D_IN], BF16, name="h_raw")
-            nc.sync.dma_start(
-                out=h_tile[:],
-                in_=H[sample, first : first + GROUP, :].rearrange("(p j) d -> p j d", j=T_TILES),
-            )
-            h_raw[g] = h_tile
-
+        half = const.tile([P, T_TILES], F32)
+        nc.vector.memset(half[:], 0.5)
+        first_sigmoid = const.tile([P, 1], F32)
+        nc.scalar.activation(out=first_sigmoid[:], in_=half[:, 0:1], func=ACT.Sigmoid)
         ident = const.tile([P, P], F32)
         make_identity(nc, ident[:])
-        half = const.tile([P, 2, T_TILES], F32)
-        nc.vector.memset(half[:], 0.5)
         b_rows_bf = const.tile([P, P], BF16)
         nc.vector.memset(b_rows_bf[:], 0.0)
-        nc.scalar.dma_start(out=b_rows_bf[0:F_TILES, :], in_=proj_in_b.rearrange("(m f) -> m f", f=P))
         scale_bf = const.tile([P, 1], BF16)
         nc.scalar.dma_start(out=scale_bf[:], in_=surp_scale.partition_broadcast(P))
         bias_bf = const.tile([P, 1], BF16)
         nc.scalar.dma_start(out=bias_bf[:], in_=surp_bias.partition_broadcast(P))
-        b_rows = const.tile([P, P], F32)
-        nc.vector.tensor_copy(out=b_rows[:], in_=b_rows_bf[:])
-        b_ps = banks.tile([P, P], F32, name="bank")
-        nc.tensor.transpose(out=b_ps[:], in_=b_rows[:], identity=ident[:])
-        b_col = const.tile([P, F_TILES], F32)
-        nc.vector.tensor_copy(out=b_col[:], in_=b_ps[:, 0:F_TILES])
+        nc.scalar.dma_start(out=b_rows_bf[0:F_TILES, :], in_=proj_in_b.rearrange("(m f) -> m f", f=P))
         scale_col = const.tile([P, 1], F32)
         nc.vector.tensor_copy(out=scale_col[:], in_=scale_bf[:])
         bias_col = const.tile([P, 1], F32)
         nc.vector.tensor_copy(out=bias_col[:], in_=bias_bf[:])
+        b_col = const.tile([P, F_TILES], F32)
 
-        mag = {}
+        def spread_bias():
+            b_rows = const.tile([P, P], F32)
+            nc.vector.tensor_copy(out=b_rows[:], in_=b_rows_bf[:])
+            b_ps = banks.tile([P, P], F32, name="bank")
+            nc.tensor.transpose(out=b_ps[:], in_=b_rows[:], identity=ident[:])
+            nc.vector.tensor_copy(out=b_col[:], in_=b_ps[:, 0:F_TILES])
+
+        norm2 = {}
         root_gate = {}
         gate_rows = {}
         h_mx = {}
@@ -104,30 +128,36 @@ def tile_proceduralmemory_pa_t_kernel(
         acc = {}
         g_rows = {}
 
-        def gate_step(g_new, g_old):
-            radicands = small.tile([P, 2, T_TILES], F32, name="radicands")
-            roots = small.tile([P, 2, T_TILES], F32, name="roots")
-            if live(g_new):
-                junk = work.tile([P, T_TILES, D_IN], BF16, name="junk", bufs=2)
-                for j in range(T_TILES):
-                    nc.scalar.activation(
-                        out=junk[:, j, :],
-                        in_=s_raw[g_new][:, j, :],
-                        func=ACT.Square,
-                        accum_out=radicands[:, 0, j : j + 1],
-                    )
-            if live(g_old):
-                nc.scalar.activation(
-                    out=radicands[:, 1, :],
-                    in_=mag[g_old],
-                    func=ACT.Sigmoid,
-                    bias=bias_col[:, 0:1],
-                    scale=scale_col[:, 0:1],
-                )
-            rows = slice(0 if live(g_new) else 1, 2 if live(g_old) else 1)
-            nc.gpsimd.tensor_tensor(out=roots[:, rows, :], in0=radicands[:, rows, :], in1=half[:, rows, :], op=ALU.pow)
-            mag[g_new] = roots[:, 0, :]
-            root_gate[g_old] = roots[:, 1, :]
+        def copy_from_bank(engine, out, in_):
+            if engine == "V":
+                nc.vector.tensor_copy(out=out, in_=in_)
+            else:
+                nc.scalar.copy(out=out, in_=in_)
+
+        def square(g, j):
+            if j == 0:
+                norm2[g] = small.tile([P, T_TILES], F32, name="norm2")
+            junk = work.tile([P, D_IN], BF16, name="junk", bufs=2)
+            nc.scalar.activation(
+                out=junk[:], in_=s_raw[g][:, j, :], func=ACT.Square, accum_out=norm2[g][:, j : j + 1]
+            )
+
+        def gate(g):
+            mag = small.tile([P, T_TILES], F32, name="mag")
+            nc.gpsimd.tensor_tensor(out=mag[:], in0=norm2[g][:], in1=half[:], op=ALU.pow)
+            s = small.tile([P, T_TILES], F32, name="s")
+            nc.scalar.activation(
+                out=s[:], in_=mag[:], func=ACT.Sigmoid, bias=bias_col[:, 0:1], scale=scale_col[:, 0:1]
+            )
+            root_gate[g] = small.tile([P, T_TILES], F32, name="root")
+            nc.gpsimd.tensor_tensor(out=root_gate[g][:], in0=s[:], in1=half[:], op=ALU.pow)
+
+        def gate_slot(k):
+            if 0 <= k < GROUPS * T_TILES:
+                square(k // T_TILES, k % T_TILES)
+            done = k - GATE_LAG
+            if done >= 0 and done % T_TILES == T_TILES - 1 and done // T_TILES < GROUPS:
+                gate(done // T_TILES)
 
         def gate_spread(g):
             spread_ps = banks.tile([P, T_TILES, P], F32, name="bank")
@@ -136,7 +166,7 @@ def tile_proceduralmemory_pa_t_kernel(
                     out=spread_ps[:, j, :], in_=root_gate[g][:, j : j + 1].to_broadcast([P, P]), identity=ident[:]
                 )
             rows = work.tile([P, GROUP], F32, name="gate_rows")
-            nc.scalar.copy(out=rows[:], in_=spread_ps[:].rearrange("p j n -> p (j n)"))
+            copy_from_bank(spread_engine(g), rows[:], spread_ps[:].rearrange("p j n -> p (j n)"))
             gate_rows[g] = rows
 
         def h_transpose(g):
@@ -150,9 +180,7 @@ def tile_proceduralmemory_pa_t_kernel(
                         nc.tensor.transpose(
                             out=t_ps[:, jj, u, :], in_=words[:, 2 * pair + jj, u : D_IN // 2 : 2], identity=ident[:]
                         )
-                nc.scalar.copy(
-                    out=grouped_words[:, 2 * pair : 2 * pair + 2], in_=t_ps[:].rearrange("p j u n -> p j n u")
-                )
+                copy_from_bank(h_engine(g, pair), grouped_words[:, 2 * pair : 2 * pair + 2], t_ps[:].rearrange("p j u n -> p j n u"))
             return grouped
 
         def quantise(grouped, name):
@@ -196,8 +224,7 @@ def tile_proceduralmemory_pa_t_kernel(
                         nc.tensor.transpose(
                             out=t_ps[:, mm, u, :], in_=words[:, 2 * pair + mm, u * P : (u + 1) * P], identity=ident[:]
                         )
-                copy_out = nc.vector.tensor_copy if pair == 0 else nc.scalar.copy
-                copy_out(out=grouped_words[:, 2 * pair : 2 * pair + 2], in_=t_ps[:].rearrange("p m u f -> p m f u"))
+                copy_from_bank(y_engine(g, pair), grouped_words[:, 2 * pair : 2 * pair + 2], t_ps[:].rearrange("p m u f -> p m f u"))
             return grouped
 
         def gram_width(m):
@@ -249,14 +276,19 @@ def tile_proceduralmemory_pa_t_kernel(
         def last_of_sample(g):
             return live(g) and g % GROUPS_PER_SAMPLE == GROUPS_PER_SAMPLE - 1
 
-        h_grouped = {}
-        for i in range(-3, GROUPS + 3):
-            if live(i + 2):
-                h_grouped[i + 2] = h_transpose(i + 2)
+
+        for k in range(LEAD * T_TILES):
+            gate_slot(k)
+        h_grouped = h_transpose(0)
+        spread_bias()
+        h_mx[0] = quantise(h_grouped, "h")
+        for i in range(GROUPS + 3):
+            if live(i + 1):
+                h_grouped = h_transpose(i + 1)
             if live(i):
                 gate_spread(i)
             if live(i - 1):
-                y_grouped[i - 1] = y_transpose(i - 1)
+                y_grouped = y_transpose(i - 1)
             if last_of_sample(i - 3):
                 mirror_and_store((i - 3) // GROUPS_PER_SAMPLE)
             for m in range(F_TILES):
@@ -264,11 +296,11 @@ def tile_proceduralmemory_pa_t_kernel(
                     project_pass(i, m)
                 if live(i - 2):
                     gram_pass(i - 2, m)
-            if live(i + 2):
-                h_mx[i + 2] = quantise(h_grouped[i + 2], "h")
+            if live(i + 1):
+                h_mx[i + 1] = quantise(h_grouped, "h")
             if live(i - 1):
-                y_mx[i - 1] = quantise(y_grouped[i - 1], "y")
-            if live(i + 3) or live(i + 2):
-                gate_step(i + 3, i + 2)
+                y_mx[i - 1] = quantise(y_grouped, "y")
+            for k in range((i + LEAD) * T_TILES, (i + LEAD + 1) * T_TILES):
+                gate_slot(k)
             if last_of_sample(i - 2):
                 drain()

@@ -28,8 +28,7 @@ MX_WIDTHS = (128, 256, 512)
 
 FLOPS = 2 * SAMPLES * TOKENS * D_IN * D_OUT + 2 * SAMPLES * TOKENS * D_OUT * D_OUT
 
-LEAD = 2
-GATE_LAG = 2
+H_LEAD = 1
 
 
 def spread_engine(g):
@@ -37,7 +36,7 @@ def spread_engine(g):
 
 
 def h_engine(g, pair):
-    return "V" if g < 2 or (pair == 1 and g % 2 == 1) else "S"
+    return "V" if g < 2 or pair == 0 and g % 2 == 1 else "S"
 
 
 def y_engine(g, pair):
@@ -51,7 +50,7 @@ def tile_proceduralmemory_pa_t_kernel(
     with ExitStack() as stack:
         const = stack.enter_context(tc.tile_pool(name="const", bufs=1))
         loads = stack.enter_context(tc.tile_pool(name="loads", bufs=GROUPS))
-        small = stack.enter_context(tc.tile_pool(name="small", bufs=8))
+        small = stack.enter_context(tc.tile_pool(name="small", bufs=6))
         work = stack.enter_context(tc.tile_pool(name="work", bufs=3))
         banks = stack.enter_context(tc.psum_pool(name="banks", bufs=4))
         sums = stack.enter_context(tc.psum_pool(name="sums", bufs=1))
@@ -92,10 +91,10 @@ def tile_proceduralmemory_pa_t_kernel(
             load(surprise, g, s_raw, "s_raw", 1)
             load(H, g, h_raw, "h_raw", 1)
 
-        half = const.tile([P, T_TILES], F32)
+        half = const.tile([P, 2, T_TILES], F32)
         nc.vector.memset(half[:], 0.5)
         first_sigmoid = const.tile([P, 1], F32)
-        nc.scalar.activation(out=first_sigmoid[:], in_=half[:, 0:1], func=ACT.Sigmoid)
+        nc.scalar.activation(out=first_sigmoid[:], in_=half[:, 0, 0:1], func=ACT.Sigmoid)
         ident = const.tile([P, P], F32)
         make_identity(nc, ident[:])
         b_rows_bf = const.tile([P, P], BF16)
@@ -118,7 +117,8 @@ def tile_proceduralmemory_pa_t_kernel(
             nc.tensor.transpose(out=b_ps[:], in_=b_rows[:], identity=ident[:])
             nc.vector.tensor_copy(out=b_col[:], in_=b_ps[:, 0:F_TILES])
 
-        norm2 = {}
+        radicands = {}
+        mag = {}
         root_gate = {}
         gate_rows = {}
         h_mx = {}
@@ -134,30 +134,32 @@ def tile_proceduralmemory_pa_t_kernel(
             else:
                 nc.scalar.copy(out=out, in_=in_)
 
-        def square(g, j):
-            if j == 0:
-                norm2[g] = small.tile([P, T_TILES], F32, name="norm2")
-            junk = work.tile([P, D_IN], BF16, name="junk", bufs=2)
+        def radicand_tile(g):
+            if g not in radicands:
+                radicands[g] = small.tile([P, 2, T_TILES], F32, name="radicands")
+            return radicands[g]
+
+        def squares(g, first, last):
+            for j in range(first, last):
+                junk = work.tile([P, D_IN], BF16, name="junk", bufs=2)
+                nc.scalar.activation(
+                    out=junk[:], in_=s_raw[g][:, j, :], func=ACT.Square, accum_out=radicand_tile(g)[:, 0, j : j + 1]
+                )
+
+        def sigmoid(g):
             nc.scalar.activation(
-                out=junk[:], in_=s_raw[g][:, j, :], func=ACT.Square, accum_out=norm2[g][:, j : j + 1]
+                out=radicand_tile(g + 1)[:, 1, :], in_=mag[g], func=ACT.Sigmoid, bias=bias_col[:, 0:1], scale=scale_col[:, 0:1]
             )
 
-        def gate(g):
-            mag = small.tile([P, T_TILES], F32, name="mag")
-            nc.gpsimd.tensor_tensor(out=mag[:], in0=norm2[g][:], in1=half[:], op=ALU.pow)
-            s = small.tile([P, T_TILES], F32, name="s")
-            nc.scalar.activation(
-                out=s[:], in_=mag[:], func=ACT.Sigmoid, bias=bias_col[:, 0:1], scale=scale_col[:, 0:1]
+        def roots_of(g, first, last):
+            roots = small.tile([P, 2, T_TILES], F32, name="roots")
+            nc.gpsimd.tensor_tensor(
+                out=roots[:, first:last, :], in0=radicand_tile(g)[:, first:last, :], in1=half[:, first:last, :], op=ALU.pow
             )
-            root_gate[g] = small.tile([P, T_TILES], F32, name="root")
-            nc.gpsimd.tensor_tensor(out=root_gate[g][:], in0=s[:], in1=half[:], op=ALU.pow)
-
-        def gate_slot(k):
-            if 0 <= k < GROUPS * T_TILES:
-                square(k // T_TILES, k % T_TILES)
-            done = k - GATE_LAG
-            if done >= 0 and done % T_TILES == T_TILES - 1 and done // T_TILES < GROUPS:
-                gate(done // T_TILES)
+            if first == 0:
+                mag[g] = roots[:, 0, :]
+            if last == 2:
+                root_gate[g - 1] = roots[:, 1, :]
 
         def gate_spread(g):
             spread_ps = banks.tile([P, T_TILES, P], F32, name="bank")
@@ -277,30 +279,46 @@ def tile_proceduralmemory_pa_t_kernel(
             return live(g) and g % GROUPS_PER_SAMPLE == GROUPS_PER_SAMPLE - 1
 
 
-        for k in range(LEAD * T_TILES):
-            gate_slot(k)
-        h_grouped = h_transpose(0)
-        spread_bias()
-        h_mx[0] = quantise(h_grouped, "h")
+        squares(0, 0, 4)
+        roots_of(0, 0, 1)
+        squares(1, 0, 2)
+        sigmoid(0)
+        roots_of(1, 1, 2)
+        squares(1, 2, 4)
+        roots_of(1, 0, 1)
+        squares(2, 0, 3)
+        h_grouped = {}
+        for g in range(H_LEAD):
+            h_grouped[g] = h_transpose(g)
+            if g == 0:
+                spread_bias()
+            if g < H_LEAD - 1:
+                h_mx[g] = quantise(h_grouped[g], "h")
         for i in range(GROUPS + 3):
-            if live(i + 1):
-                h_grouped = h_transpose(i + 1)
+            if live(i + H_LEAD):
+                h_grouped[i + H_LEAD] = h_transpose(i + H_LEAD)
             if live(i):
                 gate_spread(i)
+            if live(i + H_LEAD - 1):
+                h_mx[i + H_LEAD - 1] = quantise(h_grouped[i + H_LEAD - 1], "h")
+            if live(i - 2):
+                y_mx[i - 2] = quantise(y_grouped[i - 2], "y")
+            if live(i + 1):
+                sigmoid(i + 1)
+            if live(i + 2):
+                squares(i + 2, 3, 4)
+            if live(i + 1):
+                roots_of(i + 2, 0 if live(i + 2) else 1, 2)
             if live(i - 1):
-                y_grouped = y_transpose(i - 1)
+                y_grouped[i - 1] = y_transpose(i - 1)
             if last_of_sample(i - 3):
                 mirror_and_store((i - 3) // GROUPS_PER_SAMPLE)
+            if live(i + 3):
+                squares(i + 3, 0, 3)
             for m in range(F_TILES):
                 if live(i):
                     project_pass(i, m)
                 if live(i - 2):
                     gram_pass(i - 2, m)
-            if live(i + 1):
-                h_mx[i + 1] = quantise(h_grouped, "h")
-            if live(i - 1):
-                y_mx[i - 1] = quantise(y_grouped, "y")
-            for k in range((i + LEAD) * T_TILES, (i + LEAD + 1) * T_TILES):
-                gate_slot(k)
             if last_of_sample(i - 2):
                 drain()

@@ -28,19 +28,15 @@ MX_WIDTHS = (128, 256, 512)
 
 FLOPS = 2 * SAMPLES * TOKENS * D_IN * D_OUT + 2 * SAMPLES * TOKENS * D_OUT * D_OUT
 
-H_LEAD = 1
 
-
-def spread_engine(g):
-    return "V" if g < 1 else "S"
-
-
-def h_engine(g, pair):
-    return "V" if g < 2 or pair == 0 and g % 2 == 1 else "S"
-
-
-def y_engine(g, pair):
-    return "V" if pair == 0 else "S"
+def copy_engine(kind, part, g):
+    if kind == "h" and g < 2 or kind == "gate" and g < 2:
+        return "vector"
+    if kind == "y" and g >= GROUPS - 2:
+        return "scalar" if part == 0 else "vector"
+    if kind == "y" and (part == 0 or g % 2 == 0):
+        return "vector"
+    return "scalar"
 
 
 def tile_proceduralmemory_pa_t_kernel(
@@ -56,24 +52,21 @@ def tile_proceduralmemory_pa_t_kernel(
         sums = stack.enter_context(tc.psum_pool(name="sums", bufs=1))
         stack.enter_context(tc.manual_schedule())
 
-
         h_raw = {}
         s_raw = {}
 
-        def tokens_of(array, g):
+        def load(array, g, kept, name, parts=1):
             sample, first = g // GROUPS_PER_SAMPLE, (g % GROUPS_PER_SAMPLE) * GROUP
-            return array[sample, first : first + GROUP, :].rearrange("(p j) d -> p j d", j=T_TILES)
-
-        def load(array, g, kept, name, parts):
+            tokens = array[sample, first : first + GROUP, :].rearrange("(p j) d -> p j d", j=T_TILES)
             tile = loads.tile([P, T_TILES, D_IN], BF16, name=name)
             step = T_TILES // parts
             for j in range(0, T_TILES, step):
-                nc.sync.dma_start(out=tile[:, j : j + step, :], in_=tokens_of(array, g)[:, j : j + step, :])
+                nc.sync.dma_start(out=tile[:, j : j + step, :], in_=tokens[:, j : j + step, :])
             kept[g] = tile
 
-        load(surprise, 0, s_raw, "s_raw", 2)
-        load(H, 0, h_raw, "h_raw", 1)
-        load(surprise, 1, s_raw, "s_raw", 1)
+        load(surprise, 0, s_raw, "s_raw", parts=T_TILES)
+        load(H, 0, h_raw, "h_raw")
+        load(surprise, 1, s_raw, "s_raw")
         w_scales = const.tile([P, D_OUT], U8, align_bytes=64)
         nc.vector.memset(w_scales[:].bitcast(I32), 0)
         for quadrant in range(4):
@@ -86,10 +79,10 @@ def tile_proceduralmemory_pa_t_kernel(
             out=w_codes[:].bitcast(I32),
             in_=proj_in_w_words[0].rearrange("p n t -> p (n t)").bitcast(I32),
         )
-        load(H, 1, h_raw, "h_raw", 1)
+        load(H, 1, h_raw, "h_raw")
         for g in range(2, GROUPS):
-            load(surprise, g, s_raw, "s_raw", 1)
-            load(H, g, h_raw, "h_raw", 1)
+            load(surprise, g, s_raw, "s_raw")
+            load(H, g, h_raw, "h_raw")
 
         half = const.tile([P, 2, T_TILES], F32)
         nc.vector.memset(half[:], 0.5)
@@ -121,6 +114,8 @@ def tile_proceduralmemory_pa_t_kernel(
         mag = {}
         root_gate = {}
         gate_rows = {}
+        bank = {}
+        h_grouped = {}
         h_mx = {}
         y_t = {}
         y_grouped = {}
@@ -128,8 +123,8 @@ def tile_proceduralmemory_pa_t_kernel(
         acc = {}
         g_rows = {}
 
-        def copy_from_bank(engine, out, in_):
-            if engine == "V":
+        def copy_from_bank(kind, part, g, out, in_):
+            if copy_engine(kind, part, g) == "vector":
                 nc.vector.tensor_copy(out=out, in_=in_)
             else:
                 nc.scalar.copy(out=out, in_=in_)
@@ -162,43 +157,58 @@ def tile_proceduralmemory_pa_t_kernel(
                 root_gate[g - 1] = roots[:, 1, :]
 
         def gate_spread(g):
-            spread_ps = banks.tile([P, T_TILES, P], F32, name="bank")
+            bank["gate", 0, g] = banks.tile([P, T_TILES, P], F32, name="bank")
             for j in range(T_TILES):
                 nc.tensor.transpose(
-                    out=spread_ps[:, j, :], in_=root_gate[g][:, j : j + 1].to_broadcast([P, P]), identity=ident[:]
+                    out=bank["gate", 0, g][:, j, :],
+                    in_=root_gate[g][:, j : j + 1].to_broadcast([P, P]),
+                    identity=ident[:],
                 )
-            rows = work.tile([P, GROUP], F32, name="gate_rows")
-            copy_from_bank(spread_engine(g), rows[:], spread_ps[:].rearrange("p j n -> p (j n)"))
-            gate_rows[g] = rows
 
-        def h_transpose(g):
+        def gate_copy(g):
+            gate_rows[g] = work.tile([P, GROUP], F32, name="gate_rows")
+            copy_from_bank("gate", 0, g, gate_rows[g][:], bank["gate", 0, g][:].rearrange("p j n -> p (j n)"))
+
+        def h_transpose(g, pair):
             words = h_raw[g][:].bitcast(F32)
-            grouped = work.tile([P, PACK * GROUP], BF16, name="h_grouped", align_bytes=64, bufs=2)
-            grouped_words = grouped[:].bitcast(F32).rearrange("p (j n u) -> p j n u", j=T_TILES, u=2)
-            for pair in range(T_TILES // 2):
-                t_ps = banks.tile([P, 2, 2, P], F32, name="bank")
-                for jj in range(2):
-                    for u in range(2):
-                        nc.tensor.transpose(
-                            out=t_ps[:, jj, u, :], in_=words[:, 2 * pair + jj, u : D_IN // 2 : 2], identity=ident[:]
-                        )
-                copy_from_bank(h_engine(g, pair), grouped_words[:, 2 * pair : 2 * pair + 2], t_ps[:].rearrange("p j u n -> p j n u"))
-            return grouped
+            bank["h", pair, g] = banks.tile([P, 2, 2, P], F32, name="bank")
+            for jj in range(2):
+                for u in range(2):
+                    nc.tensor.transpose(
+                        out=bank["h", pair, g][:, jj, u, :],
+                        in_=words[:, 2 * pair + jj, u : D_IN // 2 : 2],
+                        identity=ident[:],
+                    )
 
-        def quantise(grouped, name):
+        def h_copy(g, pair):
+            if pair == 0:
+                h_grouped[g] = work.tile([P, PACK * GROUP], BF16, name="h_grouped", align_bytes=64)
+            words = h_grouped[g][:].bitcast(F32).rearrange("p (j n u) -> p j n u", j=T_TILES, u=2)
+            copy_from_bank(
+                "h", pair, g, words[:, 2 * pair : 2 * pair + 2], bank["h", pair, g][:].rearrange("p j u n -> p j n u")
+            )
+
+        def mx_tiles(name):
             codes = work.tile([P, GROUP], U32, name=name + "_codes", align_bytes=64, bufs=4)
             scales = work.tile([P, GROUP], U8, name=name + "_scales", align_bytes=64, bufs=4)
-            nc.vector.quantize_mx(out=codes[:].bitcast(FP8X4), scales=scales[:], in_=grouped[:])
             return codes, scales
+
+        def quantise_columns(mx, grouped, first, last):
+            codes, scales = mx
+            nc.vector.quantize_mx(
+                out=codes[:, first:last].bitcast(FP8X4), scales=scales[:, first:last], in_=grouped[:, PACK * first : PACK * last]
+            )
+
+        def h_quantise(g):
+            h_mx[g] = mx_tiles("h")
+            quantise_columns(h_mx[g], h_grouped[g], 0, GROUP)
 
         def project_pass(g, m):
             h_codes, h_scales = h_mx[g]
-            if m == 0:
-                y_t[g] = work.tile([P, F_TILES, GROUP], BF16, name="y_t")
             f_cols = slice(m * P, (m + 1) * P)
-            pre_ps = banks.tile([P, GROUP], F32, name="bank")
+            bank["pre", m, g] = banks.tile([P, GROUP], F32, name="bank")
             nc.tensor.matmul_mx(
-                out=pre_ps[:],
+                out=bank["pre", m, g][:],
                 lhsT=w_codes[:, f_cols].bitcast(FP8X4),
                 lhsT_scale=w_scales[:, f_cols],
                 rhs=h_codes[:].bitcast(FP8X4),
@@ -206,28 +216,44 @@ def tile_proceduralmemory_pa_t_kernel(
                 start=True,
                 stop=True,
             )
+
+        def weigh(g, m):
+            if m == 0:
+                y_t[g] = work.tile([P, F_TILES, GROUP], BF16, name="y_t")
             nc.vector.scalar_tensor_tensor(
                 out=y_t[g][:, m, :],
-                in0=pre_ps[:],
+                in0=bank["pre", m, g][:],
                 scalar=b_col[:, m : m + 1],
                 in1=gate_rows[g][:],
                 op0=ALU.add,
                 op1=ALU.mult,
             )
 
-        def y_transpose(g):
+        def y_transpose(g, pair):
             words = y_t[g][:].bitcast(F32)
-            grouped = work.tile([P, PACK * D_OUT], BF16, name="y_grouped", align_bytes=64, bufs=2)
-            grouped_words = grouped[:].bitcast(F32).rearrange("p (m f u) -> p m f u", m=F_TILES, u=2)
-            for pair in range(F_TILES // 2):
-                t_ps = banks.tile([P, 2, 2, P], F32, name="bank")
-                for mm in range(2):
-                    for u in range(2):
-                        nc.tensor.transpose(
-                            out=t_ps[:, mm, u, :], in_=words[:, 2 * pair + mm, u * P : (u + 1) * P], identity=ident[:]
-                        )
-                copy_from_bank(y_engine(g, pair), grouped_words[:, 2 * pair : 2 * pair + 2], t_ps[:].rearrange("p m u f -> p m f u"))
-            return grouped
+            bank["y", pair, g] = banks.tile([P, 2, 2, P], F32, name="bank")
+            for mm in range(2):
+                for u in range(2):
+                    nc.tensor.transpose(
+                        out=bank["y", pair, g][:, mm, u, :],
+                        in_=words[:, 2 * pair + mm, u * P : (u + 1) * P],
+                        identity=ident[:],
+                    )
+
+        def y_copy(g, pair):
+            if pair == 0:
+                y_grouped[g] = work.tile([P, PACK * D_OUT], BF16, name="y_grouped", align_bytes=64, bufs=2)
+            words = y_grouped[g][:].bitcast(F32).rearrange("p (m f u) -> p m f u", m=F_TILES, u=2)
+            copy_from_bank(
+                "y", pair, g, words[:, 2 * pair : 2 * pair + 2], bank["y", pair, g][:].rearrange("p m u f -> p m f u")
+            )
+
+        def y_quantise(g):
+            y_mx[g] = mx_tiles("y")
+            halves = 2 if g == GROUPS - 1 else 1
+            width = D_OUT // halves
+            for n in range(halves):
+                quantise_columns(y_mx[g], y_grouped[g], n * width, (n + 1) * width)
 
         def gram_width(m):
             return min(w for w in MX_WIDTHS if w >= D_OUT - m * P)
@@ -249,16 +275,17 @@ def tile_proceduralmemory_pa_t_kernel(
                 stop=(step == GROUPS_PER_SAMPLE - 1),
             )
 
-        def drain():
+        def drain(sample):
             for m in range(F_TILES):
                 g_rows[m] = work.tile([P, D_OUT], F32, name="g_rows", bufs=F_TILES)
-                right = g_rows[m][:, D_OUT - gram_width(m) : D_OUT]
+                right = slice(D_OUT - gram_width(m), D_OUT)
                 if m % 2 == 0:
-                    nc.scalar.mul(out=right, in_=acc[m][:], mul=1.0 / TOKENS)
+                    nc.scalar.mul(out=g_rows[m][:, right], in_=acc[m][:], mul=1.0 / TOKENS)
                 else:
-                    nc.vector.tensor_scalar_mul(out=right, in0=acc[m][:], scalar1=1.0 / TOKENS)
+                    nc.vector.tensor_scalar_mul(out=g_rows[m][:, right], in0=acc[m][:], scalar1=1.0 / TOKENS)
+                nc.sync.dma_start(out=out[sample, m * P : (m + 1) * P, right], in_=g_rows[m][:, right])
 
-        def mirror_and_store(sample):
+        def mirror(sample):
             for m in range(F_TILES):
                 missing = (D_OUT - gram_width(m)) // P
                 if missing > 0:
@@ -267,10 +294,10 @@ def tile_proceduralmemory_pa_t_kernel(
                         nc.tensor.transpose(
                             out=mirror_ps[:, n, :], in_=g_rows[n][:, m * P : (m + 1) * P], identity=ident[:]
                         )
-                    nc.scalar.copy(
-                        out=g_rows[m][:, 0 : missing * P], in_=mirror_ps[:].rearrange("p n f -> p (n f)")
-                    )
-                nc.sync.dma_start(out=out[sample, m * P : (m + 1) * P, :], in_=g_rows[m][:])
+                    left = slice(0, missing * P)
+                    copy_out = nc.scalar.copy if m % 2 == 0 else nc.vector.tensor_copy
+                    copy_out(out=g_rows[m][:, left], in_=mirror_ps[:].rearrange("p n f -> p (n f)"))
+                    nc.sync.dma_start(out=out[sample, m * P : (m + 1) * P, left], in_=g_rows[m][:, left])
 
         def live(g):
             return 0 <= g < GROUPS
@@ -278,47 +305,61 @@ def tile_proceduralmemory_pa_t_kernel(
         def last_of_sample(g):
             return live(g) and g % GROUPS_PER_SAMPLE == GROUPS_PER_SAMPLE - 1
 
-
         squares(0, 0, 4)
         roots_of(0, 0, 1)
-        squares(1, 0, 2)
+        for pair in (0, 1):
+            h_transpose(0, pair)
+        for pair in (0, 1):
+            h_copy(0, pair)
+        squares(1, 0, 1)
         sigmoid(0)
         roots_of(1, 1, 2)
-        squares(1, 2, 4)
+        spread_bias()
+        h_quantise(0)
+        gate_spread(0)
+        gate_copy(0)
+        squares(1, 1, 4)
         roots_of(1, 0, 1)
-        squares(2, 0, 3)
-        h_grouped = {}
-        for g in range(H_LEAD):
-            h_grouped[g] = h_transpose(g)
-            if g == 0:
-                spread_bias()
-            if g < H_LEAD - 1:
-                h_mx[g] = quantise(h_grouped[g], "h")
-        for i in range(GROUPS + 3):
-            if live(i + H_LEAD):
-                h_grouped[i + H_LEAD] = h_transpose(i + H_LEAD)
-            if live(i):
-                gate_spread(i)
-            if live(i + H_LEAD - 1):
-                h_mx[i + H_LEAD - 1] = quantise(h_grouped[i + H_LEAD - 1], "h")
-            if live(i - 2):
-                y_mx[i - 2] = quantise(y_grouped[i - 2], "y")
-            if live(i + 1):
-                sigmoid(i + 1)
+        squares(2, 0, 2)
+        sigmoid(1)
+        squares(2, 2, 3)
+
+        for i in range(GROUPS + 4):
+            if 0 < i < GROUPS:
+                h_quantise(i)
             if live(i + 2):
                 squares(i + 2, 3, 4)
             if live(i + 1):
-                roots_of(i + 2, 0 if live(i + 2) else 1, 2)
+                for pair in (0, 1):
+                    h_transpose(i + 1, pair)
+                    h_copy(i + 1, pair)
+            if i == GROUPS - 1:
+                mirror(0)
             if live(i - 1):
-                y_grouped[i - 1] = y_transpose(i - 1)
-            if last_of_sample(i - 3):
-                mirror_and_store((i - 3) // GROUPS_PER_SAMPLE)
+                y_transpose(i - 1, 0)
+                y_copy(i - 1, 0)
+            if live(i - 2):
+                y_quantise(i - 2)
+            if 0 < i < GROUPS:
+                gate_spread(i)
+            if live(i - 1):
+                y_transpose(i - 1, 1)
+            if 0 < i < GROUPS:
+                gate_copy(i)
+            if live(i - 1):
+                y_copy(i - 1, 1)
+            if 0 < i < GROUPS - 1:
+                sigmoid(i + 1)
+            if live(i + 1):
+                roots_of(i + 2, 0 if live(i + 2) else 1, 2)
             if live(i + 3):
                 squares(i + 3, 0, 3)
             for m in range(F_TILES):
+                if live(i - 3):
+                    gram_pass(i - 3, m)
                 if live(i):
                     project_pass(i, m)
-                if live(i - 2):
-                    gram_pass(i - 2, m)
-            if last_of_sample(i - 2):
-                drain()
+                    weigh(i, m)
+            if last_of_sample(i - 3):
+                drain((i - 3) // GROUPS_PER_SAMPLE)
+        mirror(1)

@@ -32,9 +32,9 @@ FLOPS = 2 * SAMPLES * TOKENS * D_IN * D_OUT + 2 * SAMPLES * TOKENS * D_OUT * D_O
 def copy_engine(kind, part, g):
     if kind == "h" and g < 2 or kind == "gate" and g < 2:
         return "vector"
-    if kind == "y" and g >= GROUPS - 2:
+    if kind == "y" and g >= GROUPS - 3:
         return "scalar" if part == 0 else "vector"
-    if kind == "y" and (part == 0 or g % 2 == 0):
+    if kind == "y" and (part == 1 or g % 4 != 0):
         return "vector"
     return "scalar"
 

@@ -29,6 +29,9 @@ MX_WIDTHS = (128, 256, 512)
 FLOPS = 2 * SAMPLES * TOKENS * D_IN * D_OUT + 2 * SAMPLES * TOKENS * D_OUT * D_OUT
 
 
+WARM_TURNS = 24
+
+
 def copy_engine(kind, part, g):
     if kind == "h" and g < 2 or kind == "gate" and g < 2:
         return "vector"
@@ -97,10 +100,6 @@ def tile_proceduralmemory_pa_t_kernel(
         bias_bf = const.tile([P, 1], BF16)
         nc.scalar.dma_start(out=bias_bf[:], in_=surp_bias.partition_broadcast(P))
         nc.scalar.dma_start(out=b_rows_bf[0:F_TILES, :], in_=proj_in_b.rearrange("(m f) -> m f", f=P))
-        scale_col = const.tile([P, 1], F32)
-        nc.vector.tensor_copy(out=scale_col[:], in_=scale_bf[:])
-        bias_col = const.tile([P, 1], F32)
-        nc.vector.tensor_copy(out=bias_col[:], in_=bias_bf[:])
         b_col = const.tile([P, F_TILES], F32)
 
         def spread_bias():
@@ -139,6 +138,19 @@ def tile_proceduralmemory_pa_t_kernel(
                 junk = work.tile([P, D_IN], BF16, name="junk", bufs=2)
                 nc.scalar.activation(
                     out=junk[:], in_=s_raw[g][:, j, :], func=ACT.Square, accum_out=radicand_tile(g)[:, 0, j : j + 1]
+                )
+
+        def squares_by_vector(g, first, last):
+            for j in range(first, last):
+                junk = work.tile([P, D_IN], F32, name="vector_junk", bufs=1)
+                nc.vector.scalar_tensor_tensor(
+                    out=junk[:],
+                    in0=s_raw[g][:, j, :],
+                    scalar=1.0,
+                    in1=s_raw[g][:, j, :],
+                    op0=ALU.mult,
+                    op1=ALU.mult,
+                    accum_out=radicand_tile(g)[:, 0, j : j + 1],
                 )
 
         def sigmoid(g):
@@ -305,8 +317,16 @@ def tile_proceduralmemory_pa_t_kernel(
         def last_of_sample(g):
             return live(g) and g % GROUPS_PER_SAMPLE == GROUPS_PER_SAMPLE - 1
 
-        squares(0, 0, 4)
+        warm = banks.tile([P, T_TILES, P], F32, name="bank")
+        for n in range(WARM_TURNS):
+            nc.tensor.transpose(out=warm[:, n % T_TILES, :], in_=ident[:], identity=ident[:])
+        squares(0, 0, 2)
+        squares_by_vector(0, 2, 4)
         roots_of(0, 0, 1)
+        scale_col = const.tile([P, 1], F32)
+        nc.vector.tensor_copy(out=scale_col[:], in_=scale_bf[:])
+        bias_col = const.tile([P, 1], F32)
+        nc.vector.tensor_copy(out=bias_col[:], in_=bias_bf[:])
         for pair in (0, 1):
             h_transpose(0, pair)
         for pair in (0, 1):

from contextlib import ExitStack

import concourse.mybir as mybir
from concourse.masks import make_identity

F32 = mybir.dt.float32
BF16 = mybir.dt.bfloat16
I32 = mybir.dt.int32
U32 = mybir.dt.uint32
U8 = mybir.dt.uint8
FP8X4 = mybir.dt.float8_e4m3fn_x4
ALU = mybir.AluOpType
ACT = mybir.ActivationFunctionType

P = 128
PACK = 4
K_PASS = P * PACK
SAMPLES = 2
TOKENS = 4096
D_IN = 512
D_OUT = 512
F_TILES = D_OUT // P
GROUP = K_PASS
T_TILES = GROUP // P
GROUPS_PER_SAMPLE = TOKENS // GROUP
GROUPS = SAMPLES * GROUPS_PER_SAMPLE
MX_WIDTHS = (128, 256, 512)

FLOPS = 2 * SAMPLES * TOKENS * D_IN * D_OUT + 2 * SAMPLES * TOKENS * D_OUT * D_OUT


WARM_TURNS = 24


def copy_engine(kind, part, g):
    if kind == "h" and g < 2 or kind == "gate" and g < 2:
        return "vector"
    if kind == "y" and g >= GROUPS - 3:
        return "scalar" if part == 0 else "vector"
    if kind == "y" and (part == 1 or g % 4 != 0):
        return "vector"
    return "scalar"


def tile_proceduralmemory_pa_t_kernel(
    tc, H, surprise, proj_in_w_words, proj_in_w_scales, proj_in_b, surp_scale, surp_bias, out
):
    nc = tc.nc
    with ExitStack() as stack:
        const = stack.enter_context(tc.tile_pool(name="const", bufs=1))
        loads = stack.enter_context(tc.tile_pool(name="loads", bufs=GROUPS))
        small = stack.enter_context(tc.tile_pool(name="small", bufs=6))
        work = stack.enter_context(tc.tile_pool(name="work", bufs=3))
        banks = stack.enter_context(tc.psum_pool(name="banks", bufs=4))
        sums = stack.enter_context(tc.psum_pool(name="sums", bufs=1))
        stack.enter_context(tc.manual_schedule())

        h_raw = {}
        s_raw = {}

        def load(array, g, kept, name, parts=1):
            sample, first = g // GROUPS_PER_SAMPLE, (g % GROUPS_PER_SAMPLE) * GROUP
            tokens = array[sample, first : first + GROUP, :].rearrange("(p j) d -> p j d", j=T_TILES)
            tile = loads.tile([P, T_TILES, D_IN], BF16, name=name)
            step = T_TILES // parts
            for j in range(0, T_TILES, step):
                nc.sync.dma_start(out=tile[:, j : j + step, :], in_=tokens[:, j : j + step, :])
            kept[g] = tile

        load(surprise, 0, s_raw, "s_raw", parts=T_TILES)
        load(H, 0, h_raw, "h_raw")
        load(surprise, 1, s_raw, "s_raw")
        w_scales = const.tile([P, D_OUT], U8, align_bytes=64)
        nc.vector.memset(w_scales[:].bitcast(I32), 0)
        for quadrant in range(4):
            nc.sync.dma_start(
                out=w_scales[32 * quadrant : 32 * quadrant + 4, :].bitcast(I32),
                in_=proj_in_w_scales[0, 4 * quadrant : 4 * quadrant + 4, :].bitcast(I32),
            )
        w_codes = const.tile([P, D_OUT], U32, align_bytes=64)
        nc.sync.dma_start(
            out=w_codes[:].bitcast(I32),
            in_=proj_in_w_words[0].rearrange("p n t -> p (n t)").bitcast(I32),
        )
        load(H, 1, h_raw, "h_raw")
        for g in range(2, GROUPS):
            load(surprise, g, s_raw, "s_raw")
            load(H, g, h_raw, "h_raw")

        half = const.tile([P, 2, T_TILES], F32)
        nc.vector.memset(half[:], 0.5)
        first_sigmoid = const.tile([P, 1], F32)
        nc.scalar.activation(out=first_sigmoid[:], in_=half[:, 0, 0:1], func=ACT.Sigmoid)
        ident = const.tile([P, P], F32)
        make_identity(nc, ident[:])
        b_rows_bf = const.tile([P, P], BF16)
        nc.vector.memset(b_rows_bf[:], 0.0)
        scale_bf = const.tile([P, 1], BF16)
        nc.scalar.dma_start(out=scale_bf[:], in_=surp_scale.partition_broadcast(P))
        bias_bf = const.tile([P, 1], BF16)
        nc.scalar.dma_start(out=bias_bf[:], in_=surp_bias.partition_broadcast(P))
        nc.scalar.dma_start(out=b_rows_bf[0:F_TILES, :], in_=proj_in_b.rearrange("(m f) -> m f", f=P))
        b_col = const.tile([P, F_TILES], F32)

        def spread_bias():
            b_rows = const.tile([P, P], F32)
            nc.vector.tensor_copy(out=b_rows[:], in_=b_rows_bf[:])
            b_ps = banks.tile([P, P], F32, name="bank")
            nc.tensor.transpose(out=b_ps[:], in_=b_rows[:], identity=ident[:])
            nc.vector.tensor_copy(out=b_col[:], in_=b_ps[:, 0:F_TILES])

        radicands = {}
        mag = {}
        root_gate = {}
        gate_rows = {}
        bank = {}
        h_grouped = {}
        h_mx = {}
        y_t = {}
        y_grouped = {}
        y_mx = {}
        acc = {}
        g_rows = {}

        def copy_from_bank(kind, part, g, out, in_):
            if copy_engine(kind, part, g) == "vector":
                nc.vector.tensor_copy(out=out, in_=in_)
            else:
                nc.scalar.copy(out=out, in_=in_)

        def radicand_tile(g):
            if g not in radicands:
                radicands[g] = small.tile([P, 2, T_TILES], F32, name="radicands")
            return radicands[g]

        def squares(g, first, last):
            for j in range(first, last):
                junk = work.tile([P, D_IN], BF16, name="junk", bufs=2)
                nc.scalar.activation(
                    out=junk[:], in_=s_raw[g][:, j, :], func=ACT.Square, accum_out=radicand_tile(g)[:, 0, j : j + 1]
                )

        def squares_by_vector(g, first, last):
            for j in range(first, last):
                junk = work.tile([P, D_IN], F32, name="vector_junk", bufs=1)
                nc.vector.scalar_tensor_tensor(
                    out=junk[:],
                    in0=s_raw[g][:, j, :],
                    scalar=1.0,
                    in1=s_raw[g][:, j, :],
                    op0=ALU.mult,
                    op1=ALU.mult,
                    accum_out=radicand_tile(g)[:, 0, j : j + 1],
                )

        def sigmoid(g):
            nc.scalar.activation(
                out=radicand_tile(g + 1)[:, 1, :], in_=mag[g], func=ACT.Sigmoid, bias=bias_col[:, 0:1], scale=scale_col[:, 0:1]
            )

        def roots_of(g, first, last):
            roots = small.tile([P, 2, T_TILES], F32, name="roots")
            nc.gpsimd.tensor_tensor(
                out=roots[:, first:last, :], in0=radicand_tile(g)[:, first:last, :], in1=half[:, first:last, :], op=ALU.pow
            )
            if first == 0:
                mag[g] = roots[:, 0, :]
            if last == 2:
                root_gate[g - 1] = roots[:, 1, :]

        def gate_spread(g):
            bank["gate", 0, g] = banks.tile([P, T_TILES, P], F32, name="bank")
            for j in range(T_TILES):
                nc.tensor.transpose(
                    out=bank["gate", 0, g][:, j, :],
                    in_=root_gate[g][:, j : j + 1].to_broadcast([P, P]),
                    identity=ident[:],
                )

        def gate_copy(g):
            gate_rows[g] = work.tile([P, GROUP], F32, name="gate_rows")
            copy_from_bank("gate", 0, g, gate_rows[g][:], bank["gate", 0, g][:].rearrange("p j n -> p (j n)"))

        def h_transpose(g, pair):
            words = h_raw[g][:].bitcast(F32)
            bank["h", pair, g] = banks.tile([P, 2, 2, P], F32, name="bank")
            for jj in range(2):
                for u in range(2):
                    nc.tensor.transpose(
                        out=bank["h", pair, g][:, jj, u, :],
                        in_=words[:, 2 * pair + jj, u : D_IN // 2 : 2],
                        identity=ident[:],
                    )

        def h_copy(g, pair):
            if pair == 0:
                h_grouped[g] = work.tile([P, PACK * GROUP], BF16, name="h_grouped", align_bytes=64)
            words = h_grouped[g][:].bitcast(F32).rearrange("p (j n u) -> p j n u", j=T_TILES, u=2)
            copy_from_bank(
                "h", pair, g, words[:, 2 * pair : 2 * pair + 2], bank["h", pair, g][:].rearrange("p j u n -> p j n u")
            )

        def mx_tiles(name):
            codes = work.tile([P, GROUP], U32, name=name + "_codes", align_bytes=64, bufs=4)
            scales = work.tile([P, GROUP], U8, name=name + "_scales", align_bytes=64, bufs=4)
            return codes, scales

        def quantise_columns(mx, grouped, first, last):
            codes, scales = mx
            nc.vector.quantize_mx(
                out=codes[:, first:last].bitcast(FP8X4), scales=scales[:, first:last], in_=grouped[:, PACK * first : PACK * last]
            )

        def h_quantise(g):
            h_mx[g] = mx_tiles("h")
            quantise_columns(h_mx[g], h_grouped[g], 0, GROUP)

        def project_pass(g, m):
            h_codes, h_scales = h_mx[g]
            f_cols = slice(m * P, (m + 1) * P)
            bank["pre", m, g] = banks.tile([P, GROUP], F32, name="bank")
            nc.tensor.matmul_mx(
                out=bank["pre", m, g][:],
                lhsT=w_codes[:, f_cols].bitcast(FP8X4),
                lhsT_scale=w_scales[:, f_cols],
                rhs=h_codes[:].bitcast(FP8X4),
                rhs_scale=h_scales[:],
                start=True,
                stop=True,
            )

        def weigh(g, m):
            if m == 0:
                y_t[g] = work.tile([P, F_TILES, GROUP], BF16, name="y_t")
            nc.vector.scalar_tensor_tensor(
                out=y_t[g][:, m, :],
                in0=bank["pre", m, g][:],
                scalar=b_col[:, m : m + 1],
                in1=gate_rows[g][:],
                op0=ALU.add,
                op1=ALU.mult,
            )

        def y_transpose(g, pair):
            words = y_t[g][:].bitcast(F32)
            bank["y", pair, g] = banks.tile([P, 2, 2, P], F32, name="bank")
            for mm in range(2):
                for u in range(2):
                    nc.tensor.transpose(
                        out=bank["y", pair, g][:, mm, u, :],
                        in_=words[:, 2 * pair + mm, u * P : (u + 1) * P],
                        identity=ident[:],
                    )

        def y_copy(g, pair):
            if pair == 0:
                y_grouped[g] = work.tile([P, PACK * D_OUT], BF16, name="y_grouped", align_bytes=64, bufs=2)
            words = y_grouped[g][:].bitcast(F32).rearrange("p (m f u) -> p m f u", m=F_TILES, u=2)
            copy_from_bank(
                "y", pair, g, words[:, 2 * pair : 2 * pair + 2], bank["y", pair, g][:].rearrange("p m u f -> p m f u")
            )

        def y_quantise(g):
            y_mx[g] = mx_tiles("y")
            halves = 2 if g == GROUPS - 1 else 1
            width = D_OUT // halves
            for n in range(halves):
                quantise_columns(y_mx[g], y_grouped[g], n * width, (n + 1) * width)

        def gram_width(m):
            return min(w for w in MX_WIDTHS if w >= D_OUT - m * P)

        def gram_pass(g, m):
            step = g % GROUPS_PER_SAMPLE
            y_codes, y_scales = y_mx[g]
            if step == 0:
                acc[m] = sums.tile([P, gram_width(m)], F32, name="acc%d" % m)
            f_cols = slice(m * P, (m + 1) * P)
            right = slice(D_OUT - gram_width(m), D_OUT)
            nc.tensor.matmul_mx(
                out=acc[m][:],
                lhsT=y_codes[:, f_cols].bitcast(FP8X4),
                lhsT_scale=y_scales[:, f_cols],
                rhs=y_codes[:, right].bitcast(FP8X4),
                rhs_scale=y_scales[:, right],
                start=(step == 0),
                stop=(step == GROUPS_PER_SAMPLE - 1),
            )

        def drain(sample):
            for m in range(F_TILES):
                g_rows[m] = work.tile([P, D_OUT], F32, name="g_rows", bufs=F_TILES)
                right = slice(D_OUT - gram_width(m), D_OUT)
                if m % 2 == 0:
                    nc.scalar.mul(out=g_rows[m][:, right], in_=acc[m][:], mul=1.0 / TOKENS)
                else:
                    nc.vector.tensor_scalar_mul(out=g_rows[m][:, right], in0=acc[m][:], scalar1=1.0 / TOKENS)
                nc.sync.dma_start(out=out[sample, m * P : (m + 1) * P, right], in_=g_rows[m][:, right])

        def mirror(sample):
            for m in range(F_TILES):
                missing = (D_OUT - gram_width(m)) // P
                if missing > 0:
                    mirror_ps = banks.tile([P, missing, P], F32, name="bank")
                    for n in range(missing):
                        nc.tensor.transpose(
                            out=mirror_ps[:, n, :], in_=g_rows[n][:, m * P : (m + 1) * P], identity=ident[:]
                        )
                    left = slice(0, missing * P)
                    copy_out = nc.scalar.copy if m % 2 == 0 else nc.vector.tensor_copy
                    copy_out(out=g_rows[m][:, left], in_=mirror_ps[:].rearrange("p n f -> p (n f)"))
                    nc.sync.dma_start(out=out[sample, m * P : (m + 1) * P, left], in_=g_rows[m][:, left])

        def live(g):
            return 0 <= g < GROUPS

        def last_of_sample(g):
            return live(g) and g % GROUPS_PER_SAMPLE == GROUPS_PER_SAMPLE - 1

        warm = banks.tile([P, T_TILES, P], F32, name="bank")
        for n in range(WARM_TURNS):
            nc.tensor.transpose(out=warm[:, n % T_TILES, :], in_=ident[:], identity=ident[:])
        squares(0, 0, 2)
        squares_by_vector(0, 2, 4)
        roots_of(0, 0, 1)
        scale_col = const.tile([P, 1], F32)
        nc.vector.tensor_copy(out=scale_col[:], in_=scale_bf[:])
        bias_col = const.tile([P, 1], F32)
        nc.vector.tensor_copy(out=bias_col[:], in_=bias_bf[:])
        for pair in (0, 1):
            h_transpose(0, pair)
        for pair in (0, 1):
            h_copy(0, pair)
        squares(1, 0, 1)
        sigmoid(0)
        roots_of(1, 1, 2)
        spread_bias()
        h_quantise(0)
        gate_spread(0)
        gate_copy(0)
        squares(1, 1, 4)
        roots_of(1, 0, 1)
        squares(2, 0, 2)
        sigmoid(1)
        squares(2, 2, 3)

        for i in range(GROUPS + 4):
            if 0 < i < GROUPS:
                h_quantise(i)
            if live(i + 2):
                squares(i + 2, 3, 4)
            if live(i + 1):
                for pair in (0, 1):
                    h_transpose(i + 1, pair)
                    h_copy(i + 1, pair)
            if i == GROUPS - 1:
                mirror(0)
            if live(i - 1):
                y_transpose(i - 1, 0)
                y_copy(i - 1, 0)
            if live(i - 2):
                y_quantise(i - 2)
            if 0 < i < GROUPS:
                gate_spread(i)
            if live(i - 1):
                y_transpose(i - 1, 1)
            if 0 < i < GROUPS:
                gate_copy(i)
            if live(i - 1):
                y_copy(i - 1, 1)
            if 0 < i < GROUPS - 1:
                sigmoid(i + 1)
            if live(i + 1):
                roots_of(i + 2, 0 if live(i + 2) else 1, 2)
            if live(i + 3):
                squares(i + 3, 0, 3)
            for m in range(F_TILES):
                if live(i - 3):
                    gram_pass(i - 3, m)
                if live(i):
                    project_pass(i, m)
                    weigh(i, m)
            if last_of_sample(i - 3):
                drain((i - 3) // GROUPS_PER_SAMPLE)
        mirror(1)
